import numpy as np
import ml_dtypes


def mxq(x, axis, fmt="e4m3"):
    dtype, down = {"e4m3": (ml_dtypes.float8_e4m3fn, 7), "e5m2": (ml_dtypes.float8_e5m2, 14)}[fmt]
    v = np.moveaxis(np.asarray(x, np.float32).astype(ml_dtypes.bfloat16).astype(np.float64), axis, -1)
    blocks = v.reshape(v.shape[:-1] + (-1, 32))
    amax = np.abs(blocks).max(-1, keepdims=True)
    byte = np.maximum(np.where(amax > 0, np.frexp(amax)[1] - 1 + 127, 0) - down, 1)
    scale = np.exp2(byte - 127.0)
    codes = (blocks / scale).astype(np.float32).astype(dtype).astype(np.float64)
    return np.moveaxis((codes * scale).reshape(v.shape), -1, axis)


WIDE = False


def mx_kscale(k):
    if not WIDE:
        return np.ones(k)
    levels = np.array([10, -10, 5, -5, 0])
    if k % 512:
        return np.exp2(np.random.permutation(np.resize(levels, k // 32))).repeat(32)
    a = np.empty((k // 512, 16))
    for p in range(k // 512):
        a[p, :8] = np.random.permutation(np.resize(levels, 8))
        for g in range(8):
            far = levels[np.abs(levels - a[p, g]) >= 10]
            a[p, g + 8] = far[np.random.randint(len(far))]
    return np.exp2(a.ravel()).repeat(32)


BF16 = ml_dtypes.bfloat16


def bf(x):
    return np.asarray(x, np.float32).astype(BF16)


def f64(x):
    return np.asarray(x).astype(np.float64)


B, PED, NED, CED = 1536, 320, 128, 512
Q = PED // 4
FEAT = 2 * PED + 3 * NED


def leaky(v):
    return np.where(v >= 0.0, v, 0.01 * v)


def point_enc(xy, wsx, bsx, wcx, bcx, wsy, bsy, wcy, bcy):
    x = xy[:, 0:1]
    y = xy[:, 1:2]
    return np.concatenate([np.sin(x * wsx + bsx), np.cos(x * wcx + bcx), np.sin(y * wsy + bsy), np.cos(y * wcy + bcy)], axis=-1)


def num_enc(t, w, b):
    return leaky(t[:, None] * w + b)


def draw0():
    s = np.array(mx_kscale(FEAT), dtype=np.float64)
    s[:2 * PED] = 1.0
    t = mx_kscale(CED)
    d = {'src_xy': bf(np.random.standard_normal((B, 2))), 'dst_xy': bf(np.random.standard_normal((B, 2))),
         'time_s': bf(np.random.uniform(size=B)), 'wait_src': bf(np.random.uniform(size=B)), 'wait_dst': bf(np.random.uniform(size=B))}
    for pfx in ('src', 'dst'):
        for part in ('wsx', 'bsx', 'wcx', 'bcx', 'wsy', 'bsy', 'wcy', 'bcy'):
            d[pfx + '_' + part] = bf(np.random.standard_normal(Q) * (1.0 if part[0] == 'w' else 0.1))
    for i, pfx in enumerate(('t', 'ws', 'wd')):
        sn = s[2 * PED + i * NED:2 * PED + (i + 1) * NED]
        d[pfx + '_w'] = bf(np.random.standard_normal(NED) * sn)
        d[pfx + '_b'] = bf(np.random.standard_normal(NED) * 0.1 * sn)
    d['W1'] = bf(np.random.standard_normal((FEAT, CED)) * 1.5 / np.sqrt(FEAT) / s[:, None] * t[None, :])
    d['b1'] = bf(np.random.standard_normal(CED) * 0.1 * t)
    d['W2'] = bf(np.random.standard_normal((CED, CED)) * 1.5 / np.sqrt(CED) / t[:, None])
    d['b2'] = bf(np.random.standard_normal(CED) * 0.1)
    return d


def core(src_xy, dst_xy, time_s, wait_src, wait_dst,
              src_wsx, src_bsx, src_wcx, src_bcx, src_wsy, src_bsy, src_wcy, src_bcy,
              dst_wsx, dst_bsx, dst_wcx, dst_bcx, dst_wsy, dst_bsy, dst_wcy, dst_bcy,
              t_w, t_b, ws_w, ws_b, wd_w, wd_b,
              W1, b1, W2, b2):
    feats = np.concatenate([
        point_enc(f64(src_xy), f64(src_wsx), f64(src_bsx), f64(src_wcx), f64(src_bcx),
                        f64(src_wsy), f64(src_bsy), f64(src_wcy), f64(src_bcy)),
        point_enc(f64(dst_xy), f64(dst_wsx), f64(dst_bsx), f64(dst_wcx), f64(dst_bcx),
                        f64(dst_wsy), f64(dst_bsy), f64(dst_wcy), f64(dst_bcy)),
        num_enc(f64(time_s), f64(t_w), f64(t_b)),
        num_enc(f64(wait_src), f64(ws_w), f64(ws_b)),
        num_enc(f64(wait_dst), f64(wd_w), f64(wd_b)),
    ], axis=-1)
    h = leaky((mxq(feats, 1, 'e4m3') @ mxq(f64(W1), 0, 'e4m3')) + f64(b1))
    return leaky((mxq(h, 1, 'e4m3') @ mxq(f64(W2), 0, 'e4m3')) + f64(b2))


def e4m3fn_bytes(y):
    return np.clip(np.asarray(y, np.float64), -448.0, 448.0).astype(np.float32).astype(ml_dtypes.float8_e4m3fn).view(np.uint8)


def e4m3fn_values(b):
    return np.asarray(b, np.uint8).view(ml_dtypes.float8_e4m3fn).astype(np.float64)


def setup_inputs():
    d = draw0()
    x0 = np.asarray(d['W2']).astype(np.float64)
    s = (np.max(np.abs(x0), axis=(1,), keepdims=True) / 448.0).astype(np.float32)
    out = {}
    for k, v in d.items():
        if k == 'W2':
            out['W2_bytes'] = e4m3fn_bytes(x0 / s.astype(np.float64))
            out['W2_scale'] = s
        else:
            out[k] = v
    return out


def reference(src_xy, dst_xy, time_s, wait_src, wait_dst, src_wsx, src_bsx, src_wcx, src_bcx, src_wsy, src_bsy, src_wcy, src_bcy, dst_wsx, dst_bsx, dst_wcx, dst_bcx, dst_wsy, dst_bsy, dst_wcy, dst_bcy, t_w, t_b, ws_w, ws_b, wd_w, wd_b, W1, b1, W2_bytes, W2_scale, b2):
    return core(src_xy, dst_xy, time_s, wait_src, wait_dst, src_wsx, src_bsx, src_wcx, src_bcx, src_wsy, src_bsy, src_wcy, src_bcy, dst_wsx, dst_bsx, dst_wcx, dst_bcx, dst_wsy, dst_bsy, dst_wcy, dst_bcy, t_w, t_b, ws_w, ws_b, wd_w, wd_b, W1, b1, e4m3fn_values(W2_bytes) * W2_scale.astype(np.float64), b2)

@@ -1,0 +1,384 @@
+import math
+from contextlib import ExitStack
+
+import concourse.mybir as mybir
+from concourse.masks import make_identity
+
+F32 = mybir.dt.float32
+BF16 = mybir.dt.bfloat16
+I32 = mybir.dt.int32
+U32 = mybir.dt.uint32
+U8 = mybir.dt.uint8
+FP8 = mybir.dt.float8_e4m3fn
+FP8X4 = mybir.dt.float8_e4m3fn_x4
+ACT = mybir.ActivationFunctionType
+ALU = mybir.AluOpType
+
+P = 128
+B = 1536
+C = 512
+FEAT = 1024
+NT = B // P
+G = 512
+NG = B // G
+FOLD = 384
+SLOPE = 0.01
+TURN = 2.0 * math.pi
+
+FLOPS = 2 * B * (FEAT * C + C * C)
+
+
+def tile_claimencoder_kernel(
+    tc, src_xy, dst_xy, time_s, wait_src, wait_dst,
+    src_wsx, src_bsx, src_wcx, src_bcx, src_wsy, src_bsy, src_wcy, src_bcy,
+    dst_wsx, dst_bsx, dst_wcx, dst_bcx, dst_wsy, dst_bsy, dst_wcy, dst_bcy,
+    t_w, t_b, ws_w, ws_b, wd_w, wd_b,
+    W1, b1, W2_bytes, W2_scale, b2, out,
+):
+    nc = tc.nc
+    with ExitStack() as ctx:
+        keep = ctx.enter_context(tc.tile_pool(name="keep", bufs=1))
+        work = ctx.enter_context(tc.tile_pool(name="work", bufs=2))
+        psum = ctx.enter_context(tc.psum_pool(name="psum", bufs=4))
+        ctx.enter_context(tc.manual_schedule())
+
+        rows_n = keep.tile([P, 896], BF16, name="rows_n")
+        nc.vector.memset(rows_n[:], 0.0)
+        rows_s = keep.tile([P, 640], BF16, name="rows_s")
+        nc.vector.memset(rows_s[:], 0.0)
+        nc.vector.memset(rows_s[32:33, :].rearrange("p (g h j) -> p g h j", g=4, h=2)[:, :, 1, :], 0.25)
+        ident = keep.tile([P, P], BF16, name="ident")
+        make_identity(nc, ident[:])
+        warm = keep.tile([P, 1], F32, name="warm")
+        nc.gpsimd.memset(warm[:], 0.0)
+        warm2 = keep.tile([P, 1], F32, name="warm2")
+
+        xt_t = keep.tile([P, NT], BF16, name="xt_t")
+        xt_ws = keep.tile([P, NT], BF16, name="xt_ws")
+        xt_wd = keep.tile([P, NT], BF16, name="xt_wd")
+        xt_s = keep.tile([P, NT, 2], BF16, name="xt_s")
+        xt_d = keep.tile([P, NT, 2], BF16, name="xt_d")
+        w1_raw = [keep.tile([P, 4, C], BF16, name="w1_raw%d" % i) for i in range(2)]
+        w2_raw = keep.tile([P, 4, C], U8, name="w2_raw")
+        w2_scl = keep.tile([P, 4], F32, name="w2_scl")
+        b1_t = keep.tile([P, 4], BF16, name="b1_t")
+        b2_t = keep.tile([P, C], BF16, name="b2_t")
+
+        def row(queue, rows, vec, r, at):
+            n = vec.shape[0]
+            queue.dma_start(out=rows[r:r + 1, at:at + n], in_=vec.rearrange("(o n) -> o n", o=1))
+
+        w1v = W1.rearrange("(g p t) c -> g p t c", g=2, t=4)
+        for tile, vec in ((xt_t, time_s), (xt_ws, wait_src), (xt_wd, wait_dst)):
+            nc.sync.dma_start(out=tile[:], in_=vec.rearrange("(p n) -> p n", n=NT))
+        nc.sync.dma_start(out=w1_raw[1][:], in_=w1v[1])
+        row(nc.scalar, rows_n, t_w, 0, 128)
+        row(nc.scalar, rows_n, t_b, 1, 128)
+        row(nc.scalar, rows_n, ws_w, 0, 256)
+        row(nc.scalar, rows_n, ws_b, 1, 256)
+        row(nc.gpsimd, rows_n, wd_w, 0, 384)
+        row(nc.gpsimd, rows_n, wd_b, 1, 384)
+        nc.sync.dma_start(out=xt_d[:].rearrange("p n c -> p (n c)"), in_=dst_xy.rearrange("(p n) c -> p (n c)", n=NT))
+        nc.sync.dma_start(out=xt_s[:].rearrange("p n c -> p (n c)"), in_=src_xy.rearrange("(p n) c -> p (n c)", n=NT))
+        nc.sync.dma_start(out=w2_raw[:], in_=W2_bytes.rearrange("(p t) c -> p t c", t=4))
+        nc.gpsimd.dma_start(out=w2_scl[:], in_=W2_scale.rearrange("(p t) o -> p (t o)", t=4))
+        nc.sync.dma_start(out=w1_raw[0][:], in_=w1v[0])
+        for i, (w, b) in enumerate(((dst_wsy, dst_bsy), (dst_wcy, dst_bcy))):
+            row(nc.gpsimd, rows_s, w, 0, 480 + 80 * i)
+            row(nc.gpsimd, rows_s, b, 1, 480 + 80 * i)
+        for i, (w, b) in enumerate(((src_wsx, src_bsx), (src_wcx, src_bcx), (src_wsy, src_bsy), (src_wcy, src_bcy), (dst_wsx, dst_bsx), (dst_wcx, dst_bcx))):
+            row(nc.sync, rows_s, w, 0, 80 * i)
+            row(nc.sync, rows_s, b, 1, 80 * i)
+        nc.gpsimd.dma_start(out=b1_t[:], in_=b1.rearrange("(p t) -> p t", t=4))
+        nc.gpsimd.dma_start(out=b2_t[:], in_=b2.partition_broadcast(P))
+        ident_f = keep.tile([P, P], F32, name="ident_f")
+        make_identity(nc, ident_f[:])
+
+        w1_q = [keep.tile([P, C], U32, name="w1_q%d" % i, align_bytes=64) for i in range(2)]
+        w1_s = [keep.tile([P, C], U8, name="w1_s%d" % i, align_bytes=64) for i in range(2)]
+        w1_g = [keep.tile([P, C * 4], BF16, name="w1_g%d" % i, align_bytes=64) for i in range(2)]
+        w2_q = keep.tile([P, C], U32, name="w2_q", align_bytes=64)
+        w2_s = keep.tile([P, C], U8, name="w2_s", align_bytes=64)
+        w2_b = keep.tile([P, 4, C], BF16, name="w2_b")
+        w2_g = keep.tile([P, C, 4], BF16, name="w2_g", align_bytes=64)
+
+        def w1_lay(i):
+            nc.vector.tensor_copy(out=w1_g[i][:].rearrange("p (t m j) -> p t m j", t=4, j=4), in_=w1_raw[i][:].rearrange("p j (m t) -> p t m j", t=4))
+
+        def w1_quant(i):
+            nc.vector.quantize_mx(out=w1_q[i][:].bitcast(FP8X4), scales=w1_s[i][:], in_=w1_g[i][:])
+
+        def w2_widen():
+            for t in range(4):
+                nc.scalar.activation(out=w2_b[:, t, :], in_=w2_raw[:, t, :].bitcast(FP8), func=ACT.Copy, scale=w2_scl[:, t:t + 1])
+
+        def w2_lay():
+            nc.scalar.copy(out=w2_g[:].rearrange("p (c i) t -> p c t i", i=4), in_=w2_b[:].rearrange("p t (c i) -> p c t i", i=4))
+
+        def w2_quant():
+            nc.vector.quantize_mx(out=w2_q[:].bitcast(FP8X4), scales=w2_s[:], in_=w2_g[:].rearrange("p c t -> p (c t)"))
+
+        feat = [keep.tile([P, B, 4], BF16, name="feat%d" % i, align_bytes=64) for i in range(2)]
+        feat_q = [keep.tile([P, B], U32, name="feat_q%d" % i, align_bytes=64) for i in range(2)]
+        feat_s = [keep.tile([P, B], U8, name="feat_s%d" % i, align_bytes=64) for i in range(2)]
+        fold = keep.tile([P, FOLD, 4], BF16, name="fold")
+        wb_n = keep.tile([P, 3, 4, 2], F32, name="wb_n")
+        w_s = keep.tile([P, 8], F32, name="w_s")
+        b_s = keep.tile([P, 8], F32, name="b_s")
+        c_s = keep.tile([P, 8], F32, name="c_s")
+        xn = [psum.tile([P, 8, P], BF16, name="xn%d" % i, tag="a") for i in range(2)]
+        x0 = [psum.tile([P, 8, P], BF16, name="x0%d" % i, tag="x", bufs=2) for i in range(2)]
+
+        def number_pre(i):
+            v = work.tile([P, 4, FOLD], F32, name="v", tag="v")
+            src = xn[i // 2][:, 3 * (i % 2):3 * (i % 2) + 3, :].rearrange("p n k -> p (n k)")
+            for t in range(4):
+                nc.scalar.activation(out=v[:, t, :], in_=src, func=ACT.Identity, scale=wb_n[:, i, t, 0:1], bias=wb_n[:, i, t, 1:2])
+            return v
+
+        def number_relu(i, v):
+            vv = v[:].rearrange("p t n -> p n t")
+            nc.vector.scalar_tensor_tensor(out=feat[1][:, FOLD * i:FOLD * (i + 1), :], in0=vv, scalar=SLOPE, in1=vv, op0=ALU.mult, op1=ALU.max)
+            nc.sync.dma_start(out=feat[1][32 * (i + 1):32 * (i + 2), 1152:1536, :], in_=feat[1][0:32, FOLD * i:FOLD * (i + 1), :])
+
+        def turns(xs, n, w0):
+            y = work.tile([P, 4, G], F32, name="y", tag="y")
+            for t in range(4):
+                at = 0
+                for x in xs:
+                    m = x.shape[1]
+                    nc.scalar.activation(out=y[:, t, at:at + m], in_=x, func=ACT.Identity, scale=w_s[:, w0 + t:w0 + t + 1], bias=b_s[:, w0 + t:w0 + t + 1])
+                    at += m
+            return y
+
+        def fraction(y, n):
+            k = work.tile([P, 4, G], I32, name="k", tag="k")
+            f = work.tile([P, 4, G], F32, name="f", tag="f")
+            for h in range(2):
+                nc.vector.tensor_copy(out=k[:, 2 * h:2 * h + 2, 0:n], in_=y[:, 2 * h:2 * h + 2, 0:n])
+            for h in range(2):
+                nc.vector.tensor_tensor(out=f[:, 2 * h:2 * h + 2, 0:n], in0=y[:, 2 * h:2 * h + 2, 0:n], in1=k[:, 2 * h:2 * h + 2, 0:n], op=ALU.subtract)
+            return f
+
+        def sine(dst, f, n):
+            nc.scalar.activation(
+                out=dst.rearrange("p (c i) t -> p c t i", i=4),
+                in_=f[:, :, 0:n].rearrange("p t (c i) -> p c t i", i=4), func=ACT.Sin, scale=TURN)
+
+        def quant(i, g):
+            s = slice(G * g, G * (g + 1))
+            nc.vector.quantize_mx(
+                out=feat_q[i][:, s].bitcast(FP8X4), scales=feat_s[i][:, s],
+                in_=feat[i][:, s, :].rearrange("p n t -> p (n t)"))
+
+        def feat0(g):
+            return feat[0][:, G * g:G * (g + 1), :]
+
+        def x0_of(g):
+            parts = []
+            for n0, n1 in ((4 * g, min(4 * g + 4, 6)), (max(4 * g, 6), 4 * g + 4)):
+                if n0 < n1:
+                    parts.append(x0[n0 // 6][:, n0 % 6:n0 % 6 + n1 - n0, :].rearrange("p n k -> p (n k)"))
+            return parts
+
+        hidden_q = [keep.tile([P, G], U32, name="hq%d" % g, align_bytes=64) for g in range(NG)]
+        hidden_s = [keep.tile([P, G], U8, name="hs%d" % g, align_bytes=64) for g in range(NG)]
+
+        def layer1(g):
+            s = slice(G * g, G * (g + 1))
+            accs = []
+            for t in range(4):
+                acc = psum.tile([P, G], F32, name="acc", tag="a")
+                for i in range(2):
+                    nc.tensor.matmul_mx(
+                        out=acc[:], lhsT=w1_q[i][:, P * t:P * (t + 1)].bitcast(FP8X4), lhsT_scale=w1_s[i][:, P * t:P * (t + 1)],
+                        rhs=feat_q[i][:, s].bitcast(FP8X4), rhs_scale=feat_s[i][:, s], start=(i == 0), stop=(i == 1))
+                accs.append(acc)
+            return accs
+
+        def bias1(accs):
+            v1 = work.tile([P, 4, G], F32, name="v1", tag="v1")
+            for t in range(4):
+                nc.scalar.activation(out=v1[:, t, :], in_=accs[t][:], func=ACT.Identity, bias=b1_t[:, t:t + 1])
+            return v1
+
+        def relu1(g, v1):
+            h = work.tile([P, G, 4], BF16, name="h", tag="h", align_bytes=64)
+            vv = v1[:].rearrange("p t n -> p n t")
+            nc.vector.scalar_tensor_tensor(out=h[:], in0=vv, scalar=SLOPE, in1=vv, op0=ALU.mult, op1=ALU.max)
+            return h
+
+        def quant_h(g, h):
+            nc.vector.quantize_mx(out=hidden_q[g][:].bitcast(FP8X4), scales=hidden_s[g][:], in_=h[:].rearrange("p n t -> p (n t)"))
+
+        out_v = out.rearrange("(p n) c -> p n c", n=NT)
+
+        def layer2(g, j):
+            v2 = work.tile([P, 2, C], F32, name="v2", tag="v2", bufs=3)
+            for i in range(2):
+                c0 = P * (2 * j + i)
+                acc2 = psum.tile([P, C], F32, name="acc2", tag="b", bufs=2)
+                nc.tensor.matmul_mx(
+                    out=acc2[:], lhsT=hidden_q[g][:, c0:c0 + P].bitcast(FP8X4), lhsT_scale=hidden_s[g][:, c0:c0 + P],
+                    rhs=w2_q[:].bitcast(FP8X4), rhs_scale=w2_s[:], start=True, stop=True)
+                nc.vector.tensor_tensor(out=v2[:, i, :], in0=acc2[:], in1=b2_t[:], op=ALU.add)
+            return v2
+
+        def relu2(g, j, v2):
+            o2 = work.tile([P, 2, C], F32, name="o2", tag="o2", bufs=3)
+            nc.vector.scalar_tensor_tensor(out=o2[:], in0=v2[:], scalar=SLOPE, in1=v2[:], op0=ALU.mult, op1=ALU.max)
+            n0 = 4 * g + 2 * j
+            nc.sync.dma_start(out=out_v[:, n0:n0 + 2, :], in_=o2[:])
+
+        b2_c = keep.tile([P, 4], F32, name="b2_c")
+        b2_s = keep.tile([P, 4], F32, name="b2_s")
+
+        def bias2():
+            pb = psum.tile([P, 4, 4], F32, name="pb", tag="b", bufs=2)
+            for c in range(4):
+                nc.tensor.matmul(pb[:, c, :], lhsT=b2_t[:, P * c:P * (c + 1)], rhs=pick[:], start=True, stop=True)
+            nc.vector.tensor_copy(out=b2_c[:], in_=pb[:, :, 0])
+            nc.vector.tensor_scalar(out=b2_s[:], in0=pb[:, :, 0], scalar1=SLOPE, scalar2=None, op0=ALU.mult)
+
+        def turned_mm(g, c):
+            acc = psum.tile([P, G], F32, name="acct", tag="a")
+            nc.tensor.matmul_mx(
+                out=acc[:], lhsT=w2_q[:, P * c:P * (c + 1)].bitcast(FP8X4), lhsT_scale=w2_s[:, P * c:P * (c + 1)],
+                rhs=hidden_q[g][:].bitcast(FP8X4), rhs_scale=hidden_s[g][:], start=True, stop=True)
+            low = work.tile([P, G], F32, name="low", tag="low")
+            nc.scalar.activation(out=low[:], in_=acc[:], func=ACT.Identity, scale=SLOPE, bias=b2_s[:, c:c + 1])
+            return acc, low
+
+        def turned_max(c, acc, low):
+            ot = work.tile([P, G], F32, name="ot", tag="ot")
+            nc.vector.scalar_tensor_tensor(out=ot[:], in0=acc[:], scalar=b2_c[:, c:c + 1], in1=low[:], op0=ALU.add, op1=ALU.max)
+            return ot
+
+        def turned_back(c, ot, o4):
+            back = psum.tile([P, 4, P], F32, name="back", tag="x", bufs=2)
+            for i in range(4):
+                nc.tensor.transpose(back[:, i, :], ot[:, P * i:P * (i + 1)], ident_f[:])
+            nc.scalar.copy(out=o4[:, :, P * c:P * (c + 1)], in_=back[:])
+
+        nc.scalar.activation(out=warm2[:], in_=warm[:], func=ACT.Sin)
+        pick = keep.tile([P, 4], BF16, name="pick")
+        nc.vector.tensor_copy(out=pick[:, 0:2], in_=ident[:, 0:2])
+        nc.vector.tensor_copy(out=pick[:, 2:4], in_=ident[:, 32:34])
+
+        ln = keep.tile([P, 9, P], BF16, name="ln")
+        for i, xt in enumerate((xt_t, xt_ws, xt_wd)):
+            nc.vector.tensor_copy(out=ln[:, :, 32 * (i + 1):32 * (i + 2)], in_=xt[:, 0:9].unsqueeze(2).to_broadcast([P, 9, 32]))
+            nc.vector.tensor_copy(out=ln[:, 3 * i:3 * i + 3, 0:32], in_=xt[:, 9:12].unsqueeze(2).to_broadcast([P, 3, 32]))
+        for n in range(9):
+            nc.tensor.transpose(xn[n // 6][:, n % 6, :], ln[:, n, :], ident[:])
+
+        pw = psum.tile([P, 16, 4], F32, name="pw", tag="b", bufs=2)
+        for t in range(4):
+            nc.tensor.matmul(pw[:, t, :], lhsT=rows_n[:, t:512:4], rhs=pick[:], start=True, stop=True)
+        for i in range(3):
+            for t in range(4):
+                at = 128 * (i + 1)
+                nc.tensor.matmul(pw[:, 4 + 4 * i + t, :], lhsT=rows_n[:, at + t:at + 512:4], rhs=pick[:], start=True, stop=True)
+        for i in range(3):
+            nc.vector.tensor_copy(out=wb_n[:, i], in_=pw[:, 0:4, 0:2])
+        nc.vector.tensor_copy(out=wb_n[0:32], in_=pw[0:32, 4:16, 0:2].rearrange("p (i t) c -> p i t c", i=3))
+        v = [number_pre(0)]
+        w1_lay(1)
+        w2_widen()
+        v.append(number_pre(1))
+
+        lf = keep.tile([P, 3, P], BF16, name="lf")
+        nc.vector.tensor_copy(
+            out=lf[:].rearrange("p i (q j) -> p i q j", q=4),
+            in_=xt_d[:, :, 1].rearrange("p (q i) -> p i q", q=4).unsqueeze(3).to_broadcast([P, 3, 4, 32]))
+        for n in range(3):
+            nc.tensor.transpose(xn[1][:, 3 + n, :], lf[:, n, :], ident[:])
+        w1_quant(1)
+        number_relu(0, v[0])
+
+        l0 = keep.tile([P, NT, P], BF16, name="l0")
+        nc.vector.tensor_copy(
+            out=l0[:, :, 0:80].rearrange("p n (c j) -> p n c j", c=2),
+            in_=xt_s[:].unsqueeze(3).to_broadcast([P, NT, 2, 40]))
+        nc.vector.tensor_copy(out=l0[:, :, 80:120], in_=xt_d[:, :, 0].unsqueeze(2).to_broadcast([P, NT, 40]))
+        nc.vector.tensor_copy(out=l0[:, :, 120:128], in_=xt_d[:, :, 1].unsqueeze(2).to_broadcast([P, NT, 8]))
+        for n in range(NT):
+            nc.tensor.transpose(x0[n // 6][:, n % 6, :], l0[:, n, :], ident[:])
+        v.append(number_pre(2))
+        number_relu(1, v[1])
+        w1_lay(0)
+        w1_quant(0)
+
+        fold_rows = keep.tile([P, 4, P], BF16, name="fold_rows")
+        nc.vector.tensor_copy(out=fold_rows[:], in_=rows_s[:, 512:640].unsqueeze(1).to_broadcast([P, 4, P]))
+        fr = fold_rows[:].rearrange("p q j -> p (q j)")
+
+        def sine_weights(lhs, w0):
+            ps = psum.tile([P, 4, 4], F32, name="ps", tag="b", bufs=2)
+            for t in range(4):
+                nc.tensor.matmul(ps[:, t, :], lhsT=lhs[:, t:512:4], rhs=pick[:], start=True, stop=True)
+            o = slice(w0, w0 + 4)
+            nc.vector.tensor_scalar(out=w_s[:, o], in0=ps[:, :, 0], scalar1=1.0 / TURN, scalar2=None, op0=ALU.mult)
+            nc.vector.tensor_copy(out=c_s[:, o], in_=ps[:, :, 2])
+            nc.vector.scalar_tensor_tensor(out=b_s[:, o], in0=ps[:, :, 1], scalar=1.0 / TURN, in1=c_s[:, o], op0=ALU.mult, op1=ALU.add)
+
+        sine_weights(fr, 0)
+        yf = turns([xn[1][:, 3:6, :].rearrange("p n k -> p (n k)")], FOLD, 0)
+        number_relu(2, v[2])
+        sine_weights(rows_s, 4)
+        ff = fraction(yf, FOLD)
+        y0 = turns(x0_of(0), G, 4)
+        sine(fold[:], ff, FOLD)
+        for q in range(4):
+            nc.sync.dma_start(out=feat[1][0:32, FOLD * q:FOLD * (q + 1), :], in_=fold[32 * q:32 * q + 32, :, :])
+        f0 = fraction(y0, G)
+        y1 = turns(x0_of(1), G, 4)
+        sine(feat0(0), f0, G)
+        f1 = fraction(y1, G)
+        y2 = turns(x0_of(2), G, 4)
+        quant(1, 0)
+        quant(0, 0)
+        a0 = layer1(0)
+        sine(feat0(1), f1, G)
+        f2 = fraction(y2, G)
+        v10 = bias1(a0)
+        w2_lay()
+        bias2()
+        quant(1, 1)
+        quant(0, 1)
+        a1 = layer1(1)
+        sine(feat0(2), f2, G)
+        quant(1, 2)
+        h0 = relu1(0, v10)
+        v11 = bias1(a1)
+        w2_quant()
+        quant_h(0, h0)
+        quant(0, 2)
+        h1 = relu1(1, v11)
+        v20 = layer2(0, 0)
+        quant_h(1, h1)
+        v21 = layer2(0, 1)
+        relu2(0, 0, v20)
+        a2 = layer1(2)
+        v12 = bias1(a2)
+        relu2(0, 1, v21)
+        h2 = relu1(2, v12)
+        o4 = work.tile([P, 4, C], F32, name="o4", tag="o4", bufs=1)
+        pend = []
+        quant_done = False
+        for c in range(4):
+            acc, low = turned_mm(1, c)
+            ot = turned_max(c, acc, low)
+            if c == 0:
+                quant_h(2, h2)
+            pend.append((c, ot))
+            if len(pend) > 1:
+                cc, oo = pend.pop(0)
+                turned_back(cc, oo, o4)
+        v20 = layer2(2, 0)
+        cc, oo = pend.pop(0)
+        turned_back(cc, oo, o4)
+        nc.sync.dma_start(out=out_v[:, 4:8, :], in_=o4[:])
+        v21 = layer2(2, 1)
+        relu2(2, 0, v20)
+        relu2(2, 1, v21)

@@ -25,6 +25,8 @@ FOLD = 384
 SLOPE = 0.01
 TURN = 2.0 * math.pi
 
+V_BACK = (5, 7, 9)
+
 FLOPS = 2 * B * (FEAT * C + C * C)
 
 
@@ -69,23 +71,27 @@ def tile_claimencoder_kernel(
             queue.dma_start(out=rows[r:r + 1, at:at + n], in_=vec.rearrange("(o n) -> o n", o=1))
 
         w1v = W1.rearrange("(g p t) c -> g p t c", g=2, t=4)
-        for tile, vec in ((xt_t, time_s), (xt_ws, wait_src), (xt_wd, wait_dst)):
+        def claim(tile, vec):
             nc.sync.dma_start(out=tile[:], in_=vec.rearrange("(p n) -> p n", n=NT))
-        nc.sync.dma_start(out=w1_raw[1][:], in_=w1v[1])
+
+        claim(xt_t, time_s)
+        claim(xt_ws, wait_src)
+        claim(xt_wd, wait_dst)
         row(nc.scalar, rows_n, t_w, 0, 128)
         row(nc.scalar, rows_n, t_b, 1, 128)
         row(nc.scalar, rows_n, ws_w, 0, 256)
         row(nc.scalar, rows_n, ws_b, 1, 256)
-        row(nc.gpsimd, rows_n, wd_w, 0, 384)
-        row(nc.gpsimd, rows_n, wd_b, 1, 384)
+        nc.sync.dma_start(out=w1_raw[1][:], in_=w1v[1])
+        row(nc.sync, rows_n, wd_w, 0, 384)
+        row(nc.sync, rows_n, wd_b, 1, 384)
         nc.sync.dma_start(out=xt_d[:].rearrange("p n c -> p (n c)"), in_=dst_xy.rearrange("(p n) c -> p (n c)", n=NT))
         nc.sync.dma_start(out=xt_s[:].rearrange("p n c -> p (n c)"), in_=src_xy.rearrange("(p n) c -> p (n c)", n=NT))
+        nc.sync.dma_start(out=w2_scl[:], in_=W2_scale.rearrange("(p t) o -> p (t o)", t=4))
         nc.sync.dma_start(out=w2_raw[:], in_=W2_bytes.rearrange("(p t) c -> p t c", t=4))
-        nc.gpsimd.dma_start(out=w2_scl[:], in_=W2_scale.rearrange("(p t) o -> p (t o)", t=4))
-        nc.sync.dma_start(out=w1_raw[0][:], in_=w1v[0])
         for i, (w, b) in enumerate(((dst_wsy, dst_bsy), (dst_wcy, dst_bcy))):
-            row(nc.gpsimd, rows_s, w, 0, 480 + 80 * i)
-            row(nc.gpsimd, rows_s, b, 1, 480 + 80 * i)
+            row(nc.sync, rows_s, w, 0, 480 + 80 * i)
+            row(nc.sync, rows_s, b, 1, 480 + 80 * i)
+        nc.sync.dma_start(out=w1_raw[0][:], in_=w1v[0])
         for i, (w, b) in enumerate(((src_wsx, src_bsx), (src_wcx, src_bcx), (src_wsy, src_bsy), (src_wcy, src_bcy), (dst_wsx, dst_bsx), (dst_wcx, dst_bcx))):
             row(nc.sync, rows_s, w, 0, 80 * i)
             row(nc.sync, rows_s, b, 1, 80 * i)
@@ -102,18 +108,18 @@ def tile_claimencoder_kernel(
         w2_b = keep.tile([P, 4, C], BF16, name="w2_b")
         w2_g = keep.tile([P, C, 4], BF16, name="w2_g", align_bytes=64)
 
-        def w1_lay(i):
-            nc.vector.tensor_copy(out=w1_g[i][:].rearrange("p (t m j) -> p t m j", t=4, j=4), in_=w1_raw[i][:].rearrange("p j (m t) -> p t m j", t=4))
+        def w1_lay(i, copy):
+            copy(out=w1_g[i][:].rearrange("p (t m j) -> p t m j", t=4, j=4), in_=w1_raw[i][:].rearrange("p j (m t) -> p t m j", t=4))
 
         def w1_quant(i):
             nc.vector.quantize_mx(out=w1_q[i][:].bitcast(FP8X4), scales=w1_s[i][:], in_=w1_g[i][:])
 
         def w2_widen():
             for t in range(4):
-                nc.scalar.activation(out=w2_b[:, t, :], in_=w2_raw[:, t, :].bitcast(FP8), func=ACT.Copy, scale=w2_scl[:, t:t + 1])
+                nc.vector.tensor_scalar(out=w2_b[:, t, :], in0=w2_raw[:, t, :].bitcast(FP8), scalar1=w2_scl[:, t:t + 1], scalar2=None, op0=ALU.mult)
 
         def w2_lay():
-            nc.scalar.copy(out=w2_g[:].rearrange("p (c i) t -> p c t i", i=4), in_=w2_b[:].rearrange("p t (c i) -> p c t i", i=4))
+            nc.vector.tensor_copy(out=w2_g[:].rearrange("p (c i) t -> p c t i", i=4), in_=w2_b[:].rearrange("p t (c i) -> p c t i", i=4))
 
         def w2_quant():
             nc.vector.quantize_mx(out=w2_q[:].bitcast(FP8X4), scales=w2_s[:], in_=w2_g[:].rearrange("p c t -> p (c t)"))
@@ -127,7 +133,7 @@ def tile_claimencoder_kernel(
         b_s = keep.tile([P, 8], F32, name="b_s")
         c_s = keep.tile([P, 8], F32, name="c_s")
         xn = [psum.tile([P, 8, P], BF16, name="xn%d" % i, tag="a") for i in range(2)]
-        x0 = [psum.tile([P, 8, P], BF16, name="x0%d" % i, tag="x", bufs=2) for i in range(2)]
+        x0 = [psum.tile([P, 8, P], BF16, name="x0%d" % i, tag="x") for i in range(2)]
 
         def number_pre(i):
             v = work.tile([P, 4, FOLD], F32, name="v", tag="v")
@@ -141,14 +147,10 @@ def tile_claimencoder_kernel(
             nc.vector.scalar_tensor_tensor(out=feat[1][:, FOLD * i:FOLD * (i + 1), :], in0=vv, scalar=SLOPE, in1=vv, op0=ALU.mult, op1=ALU.max)
             nc.sync.dma_start(out=feat[1][32 * (i + 1):32 * (i + 2), 1152:1536, :], in_=feat[1][0:32, FOLD * i:FOLD * (i + 1), :])
 
-        def turns(xs, n, w0):
+        def turns(x, n, w0):
             y = work.tile([P, 4, G], F32, name="y", tag="y")
             for t in range(4):
-                at = 0
-                for x in xs:
-                    m = x.shape[1]
-                    nc.scalar.activation(out=y[:, t, at:at + m], in_=x, func=ACT.Identity, scale=w_s[:, w0 + t:w0 + t + 1], bias=b_s[:, w0 + t:w0 + t + 1])
-                    at += m
+                nc.scalar.activation(out=y[:, t, 0:n], in_=x, func=ACT.Identity, scale=w_s[:, w0 + t:w0 + t + 1], bias=b_s[:, w0 + t:w0 + t + 1])
             return y
 
         def fraction(y, n):
@@ -175,11 +177,7 @@ def tile_claimencoder_kernel(
             return feat[0][:, G * g:G * (g + 1), :]
 
         def x0_of(g):
-            parts = []
-            for n0, n1 in ((4 * g, min(4 * g + 4, 6)), (max(4 * g, 6), 4 * g + 4)):
-                if n0 < n1:
-                    parts.append(x0[n0 // 6][:, n0 % 6:n0 % 6 + n1 - n0, :].rearrange("p n k -> p (n k)"))
-            return parts
+            return x0[g // 2][:, 4 * (g % 2):4 * (g % 2) + 4, :].rearrange("p n k -> p (n k)")
 
         hidden_q = [keep.tile([P, G], U32, name="hq%d" % g, align_bytes=64) for g in range(NG)]
         hidden_s = [keep.tile([P, G], U8, name="hs%d" % g, align_bytes=64) for g in range(NG)]
@@ -213,57 +211,44 @@ def tile_claimencoder_kernel(
 
         out_v = out.rearrange("(p n) c -> p n c", n=NT)
 
-        def layer2(g, j):
-            v2 = work.tile([P, 2, C], F32, name="v2", tag="v2", bufs=3)
-            for i in range(2):
-                c0 = P * (2 * j + i)
-                acc2 = psum.tile([P, C], F32, name="acc2", tag="b", bufs=2)
-                nc.tensor.matmul_mx(
-                    out=acc2[:], lhsT=hidden_q[g][:, c0:c0 + P].bitcast(FP8X4), lhsT_scale=hidden_s[g][:, c0:c0 + P],
-                    rhs=w2_q[:].bitcast(FP8X4), rhs_scale=w2_s[:], start=True, stop=True)
-                nc.vector.tensor_tensor(out=v2[:, i, :], in0=acc2[:], in1=b2_t[:], op=ALU.add)
-            return v2
-
-        def relu2(g, j, v2):
-            o2 = work.tile([P, 2, C], F32, name="o2", tag="o2", bufs=3)
-            nc.vector.scalar_tensor_tensor(out=o2[:], in0=v2[:], scalar=SLOPE, in1=v2[:], op0=ALU.mult, op1=ALU.max)
-            n0 = 4 * g + 2 * j
-            nc.sync.dma_start(out=out_v[:, n0:n0 + 2, :], in_=o2[:])
-
         b2_c = keep.tile([P, 4], F32, name="b2_c")
         b2_s = keep.tile([P, 4], F32, name="b2_s")
 
         def bias2():
-            pb = psum.tile([P, 4, 4], F32, name="pb", tag="b", bufs=2)
+            pb = psum.tile([P, 4, 4], F32, name="pb", tag="x")
             for c in range(4):
                 nc.tensor.matmul(pb[:, c, :], lhsT=b2_t[:, P * c:P * (c + 1)], rhs=pick[:], start=True, stop=True)
             nc.vector.tensor_copy(out=b2_c[:], in_=pb[:, :, 0])
             nc.vector.tensor_scalar(out=b2_s[:], in0=pb[:, :, 0], scalar1=SLOPE, scalar2=None, op0=ALU.mult)
 
         def turned_mm(g, c):
-            acc = psum.tile([P, G], F32, name="acct", tag="a")
+            acc = psum.tile([P, G], F32, name="acct", tag="x")
             nc.tensor.matmul_mx(
                 out=acc[:], lhsT=w2_q[:, P * c:P * (c + 1)].bitcast(FP8X4), lhsT_scale=w2_s[:, P * c:P * (c + 1)],
                 rhs=hidden_q[g][:].bitcast(FP8X4), rhs_scale=hidden_s[g][:], start=True, stop=True)
-            low = work.tile([P, G], F32, name="low", tag="low")
+            return acc
+
+        def turned_low(c, acc):
+            low = work.tile([P, G], F32, name="low", tag="low", bufs=8)
             nc.scalar.activation(out=low[:], in_=acc[:], func=ACT.Identity, scale=SLOPE, bias=b2_s[:, c:c + 1])
-            return acc, low
+            return low
 
         def turned_max(c, acc, low):
-            ot = work.tile([P, G], F32, name="ot", tag="ot")
+            ot = work.tile([P, G], F32, name="ot", tag="ot", bufs=8)
             nc.vector.scalar_tensor_tensor(out=ot[:], in0=acc[:], scalar=b2_c[:, c:c + 1], in1=low[:], op0=ALU.add, op1=ALU.max)
             return ot
 
-        def turned_back(c, ot, o4):
-            back = psum.tile([P, 4, P], F32, name="back", tag="x", bufs=2)
+        def turned_back(c, ot, o4, copy):
+            back = psum.tile([P, 4, P], F32, name="back", tag="a")
             for i in range(4):
                 nc.tensor.transpose(back[:, i, :], ot[:, P * i:P * (i + 1)], ident_f[:])
-            nc.scalar.copy(out=o4[:, :, P * c:P * (c + 1)], in_=back[:])
+            copy(out=o4[:, :, P * c:P * (c + 1)], in_=back[:])
 
         nc.scalar.activation(out=warm2[:], in_=warm[:], func=ACT.Sin)
         pick = keep.tile([P, 4], BF16, name="pick")
         nc.vector.tensor_copy(out=pick[:, 0:2], in_=ident[:, 0:2])
         nc.vector.tensor_copy(out=pick[:, 2:4], in_=ident[:, 32:34])
+        vcopy, scopy = nc.vector.tensor_copy, nc.scalar.copy
 
         ln = keep.tile([P, 9, P], BF16, name="ln")
         for i, xt in enumerate((xt_t, xt_ws, xt_wd)):
@@ -271,21 +256,22 @@ def tile_claimencoder_kernel(
             nc.vector.tensor_copy(out=ln[:, 3 * i:3 * i + 3, 0:32], in_=xt[:, 9:12].unsqueeze(2).to_broadcast([P, 3, 32]))
         for n in range(9):
             nc.tensor.transpose(xn[n // 6][:, n % 6, :], ln[:, n, :], ident[:])
+        w1_lay(1, vcopy)
 
-        pw = psum.tile([P, 16, 4], F32, name="pw", tag="b", bufs=2)
+        pw = psum.tile([P, 16, 4], F32, name="pw", tag="x")
         for t in range(4):
             nc.tensor.matmul(pw[:, t, :], lhsT=rows_n[:, t:512:4], rhs=pick[:], start=True, stop=True)
         for i in range(3):
             for t in range(4):
                 at = 128 * (i + 1)
                 nc.tensor.matmul(pw[:, 4 + 4 * i + t, :], lhsT=rows_n[:, at + t:at + 512:4], rhs=pick[:], start=True, stop=True)
-        for i in range(3):
-            nc.vector.tensor_copy(out=wb_n[:, i], in_=pw[:, 0:4, 0:2])
-        nc.vector.tensor_copy(out=wb_n[0:32], in_=pw[0:32, 4:16, 0:2].rearrange("p (i t) c -> p i t c", i=3))
+        l0 = keep.tile([P, NT, P], BF16, name="l0")
+        nc.scalar.copy(out=l0[:, :, 80:120], in_=xt_d[:, :, 0].unsqueeze(2).to_broadcast([P, NT, 40]))
+        nc.scalar.copy(out=l0[:, :, 120:128], in_=xt_d[:, :, 1].unsqueeze(2).to_broadcast([P, NT, 8]))
+        nc.scalar.copy(out=wb_n[:], in_=pw[:, 0:4, 0:2].unsqueeze(1).to_broadcast([P, 3, 4, 2]))
+        nc.scalar.copy(out=wb_n[0:32], in_=pw[0:32, 4:16, 0:2].rearrange("p (i t) c -> p i t c", i=3))
         v = [number_pre(0)]
-        w1_lay(1)
-        w2_widen()
-        v.append(number_pre(1))
+        w1_quant(1)
 
         lf = keep.tile([P, 3, P], BF16, name="lf")
         nc.vector.tensor_copy(
@@ -293,47 +279,46 @@ def tile_claimencoder_kernel(
             in_=xt_d[:, :, 1].rearrange("p (q i) -> p i q", q=4).unsqueeze(3).to_broadcast([P, 3, 4, 32]))
         for n in range(3):
             nc.tensor.transpose(xn[1][:, 3 + n, :], lf[:, n, :], ident[:])
-        w1_quant(1)
-        number_relu(0, v[0])
-
-        l0 = keep.tile([P, NT, P], BF16, name="l0")
         nc.vector.tensor_copy(
             out=l0[:, :, 0:80].rearrange("p n (c j) -> p n c j", c=2),
             in_=xt_s[:].unsqueeze(3).to_broadcast([P, NT, 2, 40]))
-        nc.vector.tensor_copy(out=l0[:, :, 80:120], in_=xt_d[:, :, 0].unsqueeze(2).to_broadcast([P, NT, 40]))
-        nc.vector.tensor_copy(out=l0[:, :, 120:128], in_=xt_d[:, :, 1].unsqueeze(2).to_broadcast([P, NT, 8]))
         for n in range(NT):
-            nc.tensor.transpose(x0[n // 6][:, n % 6, :], l0[:, n, :], ident[:])
-        v.append(number_pre(2))
-        number_relu(1, v[1])
-        w1_lay(0)
-        w1_quant(0)
+            nc.tensor.transpose(x0[n // 8][:, n % 8, :], l0[:, n, :], ident[:])
+        v.append(number_pre(1))
 
         fold_rows = keep.tile([P, 4, P], BF16, name="fold_rows")
-        nc.vector.tensor_copy(out=fold_rows[:], in_=rows_s[:, 512:640].unsqueeze(1).to_broadcast([P, 4, P]))
         fr = fold_rows[:].rearrange("p q j -> p (q j)")
 
         def sine_weights(lhs, w0):
-            ps = psum.tile([P, 4, 4], F32, name="ps", tag="b", bufs=2)
+            ps = psum.tile([P, 4, 4], F32, name="ps", tag="x")
             for t in range(4):
                 nc.tensor.matmul(ps[:, t, :], lhsT=lhs[:, t:512:4], rhs=pick[:], start=True, stop=True)
             o = slice(w0, w0 + 4)
-            nc.vector.tensor_scalar(out=w_s[:, o], in0=ps[:, :, 0], scalar1=1.0 / TURN, scalar2=None, op0=ALU.mult)
             nc.vector.tensor_copy(out=c_s[:, o], in_=ps[:, :, 2])
+            nc.vector.tensor_scalar(out=w_s[:, o], in0=ps[:, :, 0], scalar1=1.0 / TURN, scalar2=None, op0=ALU.mult)
             nc.vector.scalar_tensor_tensor(out=b_s[:, o], in0=ps[:, :, 1], scalar=1.0 / TURN, in1=c_s[:, o], op0=ALU.mult, op1=ALU.add)
 
+        nc.vector.tensor_copy(out=fold_rows[:], in_=rows_s[:, 512:640].unsqueeze(1).to_broadcast([P, 4, P]))
+        w2_widen()
         sine_weights(fr, 0)
-        yf = turns([xn[1][:, 3:6, :].rearrange("p n k -> p (n k)")], FOLD, 0)
-        number_relu(2, v[2])
+        number_relu(0, v[0])
+        yf = turns(xn[1][:, 3:6, :].rearrange("p n k -> p (n k)"), FOLD, 0)
+        number_relu(1, v[1])
+        w1_lay(0, scopy)
         sine_weights(rows_s, 4)
         ff = fraction(yf, FOLD)
         y0 = turns(x0_of(0), G, 4)
+        v.append(number_pre(2))
+        w2_lay()
         sine(fold[:], ff, FOLD)
+        f0 = fraction(y0, G)
+        number_relu(2, v[2])
         for q in range(4):
             nc.sync.dma_start(out=feat[1][0:32, FOLD * q:FOLD * (q + 1), :], in_=fold[32 * q:32 * q + 32, :, :])
-        f0 = fraction(y0, G)
+        w1_quant(0)
         y1 = turns(x0_of(1), G, 4)
         sine(feat0(0), f0, G)
+        w2_quant()
         f1 = fraction(y1, G)
         y2 = turns(x0_of(2), G, 4)
         quant(1, 0)
@@ -342,43 +327,55 @@ def tile_claimencoder_kernel(
         sine(feat0(1), f1, G)
         f2 = fraction(y2, G)
         v10 = bias1(a0)
-        w2_lay()
         bias2()
         quant(1, 1)
         quant(0, 1)
         a1 = layer1(1)
         sine(feat0(2), f2, G)
-        quant(1, 2)
         h0 = relu1(0, v10)
         v11 = bias1(a1)
-        w2_quant()
+        quant(1, 2)
         quant_h(0, h0)
         quant(0, 2)
-        h1 = relu1(1, v11)
-        v20 = layer2(0, 0)
-        quant_h(1, h1)
-        v21 = layer2(0, 1)
-        relu2(0, 0, v20)
-        a2 = layer1(2)
-        v12 = bias1(a2)
-        relu2(0, 1, v21)
-        h2 = relu1(2, v12)
-        o4 = work.tile([P, 4, C], F32, name="o4", tag="o4", bufs=1)
-        pend = []
-        quant_done = False
+        o4 = [work.tile([P, 4, C], F32, name="o4_%d" % g, tag="o4", bufs=3) for g in range(NG)]
+
+        ac = [[None] * 4 for g in range(NG)]
+        lo = [[None] * 4 for g in range(NG)]
+        ot = [[None] * 4 for g in range(NG)]
+
+        def mm(g, c):
+            ac[g][c] = turned_mm(g, c)
+
+        def low(g, c):
+            lo[g][c] = turned_low(c, ac[g][c])
+
+        def top(g, c):
+            ot[g][c] = turned_max(c, ac[g][c], lo[g][c])
+
+        def back(g, c, copy):
+            turned_back(c, ot[g][c], o4[g], copy)
+            nc.sync.dma_start(out=out_v[:, 4 * g:4 * g + 4, P * c:P * (c + 1)], in_=o4[g][:, :, P * c:P * (c + 1)])
+
         for c in range(4):
-            acc, low = turned_mm(1, c)
-            ot = turned_max(c, acc, low)
-            if c == 0:
+            mm(0, c)
+        a2 = layer1(2)
+        h1 = relu1(1, v11)
+        for c in range(4):
+            low(0, c)
+        v12 = bias1(a2)
+        units = [(g, c) for g in range(NG) for c in range(4)]
+        for s, u in enumerate(units):
+            if s == 3:
+                h2 = relu1(2, v12)
+            top(*u)
+            if s == 0:
+                quant_h(1, h1)
+            if s == 3:
                 quant_h(2, h2)
-            pend.append((c, ot))
-            if len(pend) > 1:
-                cc, oo = pend.pop(0)
-                turned_back(cc, oo, o4)
-        v20 = layer2(2, 0)
-        cc, oo = pend.pop(0)
-        turned_back(cc, oo, o4)
-        nc.sync.dma_start(out=out_v[:, 4:8, :], in_=o4[:])
-        v21 = layer2(2, 1)
-        relu2(2, 0, v20)
-        relu2(2, 1, v21)
+            if s + 4 < len(units):
+                mm(*units[s + 4])
+                low(*units[s + 4])
+            if s >= 2:
+                back(*units[s - 2], vcopy if s - 2 in V_BACK else scopy)
+        back(*units[-2], vcopy)
+        back(*units[-1], scopy)

@@ -25,7 +25,12 @@ FOLD = 384
 SLOPE = 0.01
 TURN = 2.0 * math.pi
 
-V_BACK = (5, 7, 9)
+TURNED = (0, 1,)
+LG = ((0, 512), (512, 512), (1024, 512))
+
+ORDER = """
+pick ln w2wid0 w1lay1 xn pw l0 wbn w1q1 w2wid2 frow smF b2m lf nv1 sm0 w1lay0 spF soF nr1 nv0 yF nr0 sp0 so0 w2wid3 kF y0 fF nv2 k0 y1 sF f0 nr2 k1 w1q0 s0 y2 f1 sd s1 q00 q10 b2o k2 m01 m00 q11 v00 v01 f2 m03 w2wid1 q01 m02 w2lay v02 v03 m11 h0 w2q s2 m12 qh0 v11 m10 m13 q12 tm01 tm03 v12 q02 tm00 v13 m21 v10 m22 tl03 tl00 v21 h1 tl01 m23 tm02 v22 tx03 tx01 m20 v23 tl02 qh1 tm10 v20 tm12 tx00 tx02 tl12 h2 tl10 tm13 tm11 tb01 tb00 to01 tb03 tx10 tb02 to00 tl11 qh2 tx12 nm21 tl13 nm22 to03 tx11 tx13 tb13 to02 na21 to13 tb10 na22 to10 nm23 tb12 nm20 no21 tb11 to12 na23 no22 na20 to11 no23 no20
+"""
 
 FLOPS = 2 * B * (FEAT * C + C * C)
 
@@ -55,9 +60,7 @@ def tile_claimencoder_kernel(
         nc.gpsimd.memset(warm[:], 0.0)
         warm2 = keep.tile([P, 1], F32, name="warm2")
 
-        xt_t = keep.tile([P, NT], BF16, name="xt_t")
-        xt_ws = keep.tile([P, NT], BF16, name="xt_ws")
-        xt_wd = keep.tile([P, NT], BF16, name="xt_wd")
+        xt_n = keep.tile([P, 3, 16], BF16, name="xt_n")
         xt_s = keep.tile([P, NT, 2], BF16, name="xt_s")
         xt_d = keep.tile([P, NT, 2], BF16, name="xt_d")
         w1_raw = [keep.tile([P, 4, C], BF16, name="w1_raw%d" % i) for i in range(2)]
@@ -71,12 +74,8 @@ def tile_claimencoder_kernel(
             queue.dma_start(out=rows[r:r + 1, at:at + n], in_=vec.rearrange("(o n) -> o n", o=1))
 
         w1v = W1.rearrange("(g p t) c -> g p t c", g=2, t=4)
-        def claim(tile, vec):
-            nc.sync.dma_start(out=tile[:], in_=vec.rearrange("(p n) -> p n", n=NT))
-
-        claim(xt_t, time_s)
-        claim(xt_ws, wait_src)
-        claim(xt_wd, wait_dst)
+        for i, vec in enumerate((time_s, wait_src, wait_dst)):
+            nc.sync.dma_start(out=xt_n[:, i, 0:NT], in_=vec.rearrange("(p n) -> p n", n=NT))
         row(nc.scalar, rows_n, t_w, 0, 128)
         row(nc.scalar, rows_n, t_b, 1, 128)
         row(nc.scalar, rows_n, ws_w, 0, 256)
@@ -84,14 +83,14 @@ def tile_claimencoder_kernel(
         nc.sync.dma_start(out=w1_raw[1][:], in_=w1v[1])
         row(nc.sync, rows_n, wd_w, 0, 384)
         row(nc.sync, rows_n, wd_b, 1, 384)
-        nc.sync.dma_start(out=xt_d[:].rearrange("p n c -> p (n c)"), in_=dst_xy.rearrange("(p n) c -> p (n c)", n=NT))
-        nc.sync.dma_start(out=xt_s[:].rearrange("p n c -> p (n c)"), in_=src_xy.rearrange("(p n) c -> p (n c)", n=NT))
         nc.sync.dma_start(out=w2_scl[:], in_=W2_scale.rearrange("(p t) o -> p (t o)", t=4))
         nc.sync.dma_start(out=w2_raw[:], in_=W2_bytes.rearrange("(p t) c -> p t c", t=4))
+        nc.sync.dma_start(out=xt_d[:].rearrange("p n c -> p (n c)"), in_=dst_xy.rearrange("(p n) c -> p (n c)", n=NT))
+        nc.sync.dma_start(out=xt_s[:].rearrange("p n c -> p (n c)"), in_=src_xy.rearrange("(p n) c -> p (n c)", n=NT))
+        nc.sync.dma_start(out=w1_raw[0][:], in_=w1v[0])
         for i, (w, b) in enumerate(((dst_wsy, dst_bsy), (dst_wcy, dst_bcy))):
             row(nc.sync, rows_s, w, 0, 480 + 80 * i)
             row(nc.sync, rows_s, b, 1, 480 + 80 * i)
-        nc.sync.dma_start(out=w1_raw[0][:], in_=w1v[0])
         for i, (w, b) in enumerate(((src_wsx, src_bsx), (src_wcx, src_bcx), (src_wsy, src_bsy), (src_wcy, src_bcy), (dst_wsx, dst_bsx), (dst_wcx, dst_bcx))):
             row(nc.sync, rows_s, w, 0, 80 * i)
             row(nc.sync, rows_s, b, 1, 80 * i)
@@ -99,6 +98,9 @@ def tile_claimencoder_kernel(
         nc.gpsimd.dma_start(out=b2_t[:], in_=b2.partition_broadcast(P))
         ident_f = keep.tile([P, P], F32, name="ident_f")
         make_identity(nc, ident_f[:])
+
+        vec, sca, pe = nc.vector, nc.scalar, nc.tensor
+        S = {}
 
         w1_q = [keep.tile([P, C], U32, name="w1_q%d" % i, align_bytes=64) for i in range(2)]
         w1_s = [keep.tile([P, C], U8, name="w1_s%d" % i, align_bytes=64) for i in range(2)]
@@ -111,18 +113,17 @@ def tile_claimencoder_kernel(
         def w1_lay(i, copy):
             copy(out=w1_g[i][:].rearrange("p (t m j) -> p t m j", t=4, j=4), in_=w1_raw[i][:].rearrange("p j (m t) -> p t m j", t=4))
 
-        def w1_quant(i):
-            nc.vector.quantize_mx(out=w1_q[i][:].bitcast(FP8X4), scales=w1_s[i][:], in_=w1_g[i][:])
+        S["w1lay1"] = lambda: w1_lay(1, vec.tensor_copy)
+        S["w1lay0"] = lambda: w1_lay(0, vec.tensor_copy)
+        for i in range(2):
+            S["w1q%d" % i] = lambda i=i: vec.quantize_mx(out=w1_q[i][:].bitcast(FP8X4), scales=w1_s[i][:], in_=w1_g[i][:])
 
-        def w2_widen():
-            for t in range(4):
-                nc.vector.tensor_scalar(out=w2_b[:, t, :], in0=w2_raw[:, t, :].bitcast(FP8), scalar1=w2_scl[:, t:t + 1], scalar2=None, op0=ALU.mult)
-
-        def w2_lay():
-            nc.vector.tensor_copy(out=w2_g[:].rearrange("p (c i) t -> p c t i", i=4), in_=w2_b[:].rearrange("p t (c i) -> p c t i", i=4))
-
-        def w2_quant():
-            nc.vector.quantize_mx(out=w2_q[:].bitcast(FP8X4), scales=w2_s[:], in_=w2_g[:].rearrange("p c t -> p (c t)"))
+        def w2_widen(t):
+            sca.activation(out=w2_b[:, t, :], in_=w2_raw[:, t, :].bitcast(FP8), func=ACT.Copy, scale=w2_scl[:, t:t + 1])
+        for t in range(4):
+            S["w2wid%d" % t] = lambda t=t: w2_widen(t)
+        S["w2lay"] = lambda: vec.tensor_copy(out=w2_g[:].rearrange("p (c i) t -> p c t i", i=4), in_=w2_b[:].rearrange("p t (c i) -> p c t i", i=4))
+        S["w2q"] = lambda: vec.quantize_mx(out=w2_q[:].bitcast(FP8X4), scales=w2_s[:], in_=w2_g[:].rearrange("p c t -> p (c t)"))
 
         feat = [keep.tile([P, B, 4], BF16, name="feat%d" % i, align_bytes=64) for i in range(2)]
         feat_q = [keep.tile([P, B], U32, name="feat_q%d" % i, align_bytes=64) for i in range(2)]
@@ -132,250 +133,273 @@ def tile_claimencoder_kernel(
         w_s = keep.tile([P, 8], F32, name="w_s")
         b_s = keep.tile([P, 8], F32, name="b_s")
         c_s = keep.tile([P, 8], F32, name="c_s")
-        xn = [psum.tile([P, 8, P], BF16, name="xn%d" % i, tag="a") for i in range(2)]
-        x0 = [psum.tile([P, 8, P], BF16, name="x0%d" % i, tag="x") for i in range(2)]
+        pick = keep.tile([P, 4], BF16, name="pick")
+        ln = keep.tile([P, 9, P], BF16, name="ln")
+        lf = keep.tile([P, 3, P], BF16, name="lf")
+        l0 = keep.tile([P, NT, P], BF16, name="l0")
+        fold_rows = keep.tile([P, 4, P], BF16, name="fold_rows")
+        fr = fold_rows[:].rearrange("p q j -> p (q j)")
+        M = {}
 
-        def number_pre(i):
-            v = work.tile([P, 4, FOLD], F32, name="v", tag="v")
-            src = xn[i // 2][:, 3 * (i % 2):3 * (i % 2) + 3, :].rearrange("p n k -> p (n k)")
+        def pick_step():
+            nc.gpsimd.tensor_copy(out=pick[:, 0:2], in_=ident[:, 0:2])
+            nc.gpsimd.tensor_copy(out=pick[:, 2:4], in_=ident[:, 32:34])
+        S["pick"] = pick_step
+
+        def ln_step():
+            vec.tensor_copy(
+                out=ln[:, :, 32:128].rearrange("p n (i j) -> p n i j", i=3),
+                in_=xt_n[:, :, 0:9].rearrange("p i n -> p n i").unsqueeze(3).to_broadcast([P, 9, 3, 32]))
+            vec.tensor_copy(
+                out=ln[:, :, 0:32].rearrange("p (i n) j -> p i n j", i=3),
+                in_=xt_n[:, :, 9:12].unsqueeze(3).to_broadcast([P, 3, 3, 32]))
+        S["ln"] = ln_step
+
+        def xn_step():
+            M["xn"] = [psum.tile([P, 8, P], BF16, name="xn%d" % i, tag="a") for i in range(2)]
+            for n in range(9):
+                pe.transpose(M["xn"][n // 6][:, n % 6, :], ln[:, n, :], ident[:])
+        S["xn"] = xn_step
+
+        def lf_step():
+            vec.tensor_copy(
+                out=lf[:].rearrange("p i (q j) -> p i q j", q=4),
+                in_=xt_d[:, :, 1].rearrange("p (q i) -> p i q", q=4).unsqueeze(3).to_broadcast([P, 3, 4, 32]))
+            for n in range(3):
+                pe.transpose(M["xn"][1][:, 3 + n, :], lf[:, n, :], ident[:])
+        S["lf"] = lf_step
+
+        def l0_step():
+            vec.tensor_copy(out=l0[:, :, 80:120], in_=xt_d[:, :, 0].unsqueeze(2).to_broadcast([P, NT, 40]))
+            vec.tensor_copy(out=l0[:, :, 120:128], in_=xt_d[:, :, 1].unsqueeze(2).to_broadcast([P, NT, 8]))
+            vec.tensor_copy(
+                out=l0[:, :, 0:80].rearrange("p n (c j) -> p n c j", c=2),
+                in_=xt_s[:].unsqueeze(3).to_broadcast([P, NT, 2, 40]))
+            M["x0"] = [psum.tile([P, 8, P], BF16, name="x0%d" % i, tag="x") for i in range(2)]
+            for n in range(NT):
+                pe.transpose(M["x0"][n // 8][:, n % 8, :], l0[:, n, :], ident[:])
+        S["l0"] = l0_step
+
+        def pw_step():
+            pw = M["pw"] = psum.tile([P, 16, 4], F32, name="pw", tag="x")
             for t in range(4):
-                nc.scalar.activation(out=v[:, t, :], in_=src, func=ACT.Identity, scale=wb_n[:, i, t, 0:1], bias=wb_n[:, i, t, 1:2])
-            return v
+                pe.matmul(pw[:, t, :], lhsT=rows_n[:, t:512:4], rhs=pick[:], start=True, stop=True)
+            for i in range(3):
+                for t in range(4):
+                    at = 128 * (i + 1)
+                    pe.matmul(pw[:, 4 + 4 * i + t, :], lhsT=rows_n[:, at + t:at + 512:4], rhs=pick[:], start=True, stop=True)
+        S["pw"] = pw_step
 
-        def number_relu(i, v):
-            vv = v[:].rearrange("p t n -> p n t")
-            nc.vector.scalar_tensor_tensor(out=feat[1][:, FOLD * i:FOLD * (i + 1), :], in0=vv, scalar=SLOPE, in1=vv, op0=ALU.mult, op1=ALU.max)
+        def wbn_step():
+            sca.copy(out=wb_n[:], in_=M["pw"][:, 0:4, 0:2].unsqueeze(1).to_broadcast([P, 3, 4, 2]))
+            sca.copy(out=wb_n[0:32], in_=M["pw"][0:32, 4:16, 0:2].rearrange("p (i t) c -> p i t c", i=3))
+        S["wbn"] = wbn_step
+
+        def nv_step(i):
+            v = M["v", i] = work.tile([P, 4, FOLD], F32, name="v", tag="v")
+            src = M["xn"][i // 2][:, 3 * (i % 2):3 * (i % 2) + 3, :].rearrange("p n k -> p (n k)")
+            for t in range(4):
+                sca.activation(out=v[:, t, :], in_=src, func=ACT.Identity, scale=wb_n[:, i, t, 0:1], bias=wb_n[:, i, t, 1:2])
+
+        def nr_step(i):
+            vv = M["v", i][:].rearrange("p t n -> p n t")
+            vec.scalar_tensor_tensor(out=feat[1][:, FOLD * i:FOLD * (i + 1), :], in0=vv, scalar=SLOPE, in1=vv, op0=ALU.mult, op1=ALU.max)
             nc.sync.dma_start(out=feat[1][32 * (i + 1):32 * (i + 2), 1152:1536, :], in_=feat[1][0:32, FOLD * i:FOLD * (i + 1), :])
+        for i in range(3):
+            S["nv%d" % i] = lambda i=i: nv_step(i)
+            S["nr%d" % i] = lambda i=i: nr_step(i)
 
-        def turns(x, n, w0):
-            y = work.tile([P, 4, G], F32, name="y", tag="y")
+        S["frow"] = lambda: vec.tensor_copy(out=fold_rows[:], in_=rows_s[:, 512:640].unsqueeze(1).to_broadcast([P, 4, P]))
+
+        def sw_mm(w0, lhs):
+            ps = M["ps", w0] = psum.tile([P, 4, 4], F32, name="ps", tag="x")
             for t in range(4):
-                nc.scalar.activation(out=y[:, t, 0:n], in_=x, func=ACT.Identity, scale=w_s[:, w0 + t:w0 + t + 1], bias=b_s[:, w0 + t:w0 + t + 1])
-            return y
+                pe.matmul(ps[:, t, :], lhsT=lhs[:, t:512:4], rhs=pick[:], start=True, stop=True)
 
-        def fraction(y, n):
-            k = work.tile([P, 4, G], I32, name="k", tag="k")
-            f = work.tile([P, 4, G], F32, name="f", tag="f")
-            for h in range(2):
-                nc.vector.tensor_copy(out=k[:, 2 * h:2 * h + 2, 0:n], in_=y[:, 2 * h:2 * h + 2, 0:n])
-            for h in range(2):
-                nc.vector.tensor_tensor(out=f[:, 2 * h:2 * h + 2, 0:n], in0=y[:, 2 * h:2 * h + 2, 0:n], in1=k[:, 2 * h:2 * h + 2, 0:n], op=ALU.subtract)
-            return f
+        def sw_part(w0):
+            ps = M["ps", w0]
+            o = slice(w0, w0 + 4)
+            sca.copy(out=c_s[:, o], in_=ps[:, :, 2])
+            sca.activation(out=w_s[:, o], in_=ps[:, :, 0], func=ACT.Copy, scale=1.0 / TURN)
 
-        def sine(dst, f, n):
-            nc.scalar.activation(
-                out=dst.rearrange("p (c i) t -> p c t i", i=4),
-                in_=f[:, :, 0:n].rearrange("p t (c i) -> p c t i", i=4), func=ACT.Sin, scale=TURN)
+        def sw_out(w0):
+            ps = M["ps", w0]
+            o = slice(w0, w0 + 4)
+            vec.scalar_tensor_tensor(out=b_s[:, o], in0=ps[:, :, 1], scalar=1.0 / TURN, in1=c_s[:, o], op0=ALU.mult, op1=ALU.add)
+        S["smF"] = lambda: sw_mm(0, fr)
+        S["sm0"] = lambda: sw_mm(4, rows_s)
+        S["spF"] = lambda: sw_part(0)
+        S["sp0"] = lambda: sw_part(4)
+        S["soF"] = lambda: sw_out(0)
+        S["so0"] = lambda: sw_out(4)
 
-        def quant(i, g):
-            s = slice(G * g, G * (g + 1))
-            nc.vector.quantize_mx(
+        def y_step(g):
+            n, w0 = (FOLD, 0) if g == "F" else (G, 4)
+            if g == "F":
+                x = M["xn"][1][:, 3:6, :]
+            else:
+                x = M["x0"][g // 2][:, 4 * (g % 2):4 * (g % 2) + 4, :]
+            y = M["y", g] = work.tile([P, 4, G], F32, name="y", tag="y", bufs=3)
+            for t in range(4):
+                sca.activation(out=y[:, t, 0:n], in_=x.rearrange("p n k -> p (n k)"), func=ACT.Identity, scale=w_s[:, w0 + t:w0 + t + 1], bias=b_s[:, w0 + t:w0 + t + 1])
+
+        def k_step(g):
+            n = FOLD if g == "F" else G
+            k = M["k", g] = work.tile([P, 4, G], I32, name="k", tag="k")
+            vec.tensor_copy(out=k[:, :, 0:n], in_=M["y", g][:, :, 0:n])
+
+        def f_step(g):
+            n = FOLD if g == "F" else G
+            y, k = M["y", g], M["k", g]
+            vec.tensor_tensor(out=y[:, :, 0:n], in0=y[:, :, 0:n], in1=k[:, :, 0:n], op=ALU.subtract)
+
+        def sin_step(L):
+            if L == "F":
+                dst, src = fold[:], M["y", "F"][:, :, 0:FOLD]
+            else:
+                a, n = LG[L]
+                dst, src = feat[0][:, a:a + n, :], M["y", a // G][:, :, a % G:a % G + n]
+            sca.activation(
+                out=dst.rearrange("p (c i) t -> p c t i", i=4), in_=src.rearrange("p t (c i) -> p c t i", i=4), func=ACT.Sin, scale=TURN)
+
+        def move_step():
+            for q in range(4):
+                nc.sync.dma_start(out=feat[1][0:32, FOLD * q:FOLD * (q + 1), :], in_=fold[32 * q:32 * q + 32, :, :])
+        S["sd"] = move_step
+
+        def q_step(i, L):
+            s = slice(LG[L][0], LG[L][0] + LG[L][1])
+            vec.quantize_mx(
                 out=feat_q[i][:, s].bitcast(FP8X4), scales=feat_s[i][:, s],
                 in_=feat[i][:, s, :].rearrange("p n t -> p (n t)"))
 
-        def feat0(g):
-            return feat[0][:, G * g:G * (g + 1), :]
+        def m1_step(L, t):
+            a, n = LG[L]
+            s = slice(a, a + n)
+            if n == G:
+                acc = M["acc", L, t] = psum.tile([P, G], F32, name="acc", tag="a")
+            else:
+                if ("accs", L, t // 2) not in M:
+                    M["accs", L, t // 2] = psum.tile([P, 2, n], F32, name="accs", tag="a")
+                acc = M["acc", L, t] = M["accs", L, t // 2][:, t % 2, :]
+            for i in range(2):
+                pe.matmul_mx(
+                    out=acc[:, :], lhsT=w1_q[i][:, P * t:P * (t + 1)].bitcast(FP8X4), lhsT_scale=w1_s[i][:, P * t:P * (t + 1)],
+                    rhs=feat_q[i][:, s].bitcast(FP8X4), rhs_scale=feat_s[i][:, s], start=(i == 0), stop=(i == 1))
 
-        def x0_of(g):
-            return x0[g // 2][:, 4 * (g % 2):4 * (g % 2) + 4, :].rearrange("p n k -> p (n k)")
+        def v1_step(L, t):
+            if ("v1", L) not in M:
+                M["v1", L] = work.tile([P, 4, G], F32, name="v1", tag="v1", bufs=3)
+            n = LG[L][1]
+            sca.activation(out=M["v1", L][:, t, 0:n], in_=M["acc", L, t][:, :], func=ACT.Identity, bias=b1_t[:, t:t + 1])
 
-        hidden_q = [keep.tile([P, G], U32, name="hq%d" % g, align_bytes=64) for g in range(NG)]
-        hidden_s = [keep.tile([P, G], U8, name="hs%d" % g, align_bytes=64) for g in range(NG)]
+        def h_step(L):
+            n = LG[L][1]
+            h = M["h", L] = work.tile([P, G, 4], BF16, name="h", tag="h", align_bytes=64)
+            vv = M["v1", L][:, :, 0:n].rearrange("p t n -> p n t")
+            vec.scalar_tensor_tensor(out=h[:, 0:n, :], in0=vv, scalar=SLOPE, in1=vv, op0=ALU.mult, op1=ALU.max)
 
-        def layer1(g):
-            s = slice(G * g, G * (g + 1))
-            accs = []
-            for t in range(4):
-                acc = psum.tile([P, G], F32, name="acc", tag="a")
-                for i in range(2):
-                    nc.tensor.matmul_mx(
-                        out=acc[:], lhsT=w1_q[i][:, P * t:P * (t + 1)].bitcast(FP8X4), lhsT_scale=w1_s[i][:, P * t:P * (t + 1)],
-                        rhs=feat_q[i][:, s].bitcast(FP8X4), rhs_scale=feat_s[i][:, s], start=(i == 0), stop=(i == 1))
-                accs.append(acc)
-            return accs
+        hidden_q = keep.tile([P, B], U32, name="hidden_q", align_bytes=64)
+        hidden_s = keep.tile([P, B], U8, name="hidden_s", align_bytes=64)
 
-        def bias1(accs):
-            v1 = work.tile([P, 4, G], F32, name="v1", tag="v1")
-            for t in range(4):
-                nc.scalar.activation(out=v1[:, t, :], in_=accs[t][:], func=ACT.Identity, bias=b1_t[:, t:t + 1])
-            return v1
-
-        def relu1(g, v1):
-            h = work.tile([P, G, 4], BF16, name="h", tag="h", align_bytes=64)
-            vv = v1[:].rearrange("p t n -> p n t")
-            nc.vector.scalar_tensor_tensor(out=h[:], in0=vv, scalar=SLOPE, in1=vv, op0=ALU.mult, op1=ALU.max)
-            return h
-
-        def quant_h(g, h):
-            nc.vector.quantize_mx(out=hidden_q[g][:].bitcast(FP8X4), scales=hidden_s[g][:], in_=h[:].rearrange("p n t -> p (n t)"))
+        def qh_step(L):
+            a, n = LG[L]
+            vec.quantize_mx(out=hidden_q[:, a:a + n].bitcast(FP8X4), scales=hidden_s[:, a:a + n], in_=M["h", L][:, 0:n, :].rearrange("p n t -> p (n t)"))
 
         out_v = out.rearrange("(p n) c -> p n c", n=NT)
-
+        o4 = keep.tile([P, NT, C], F32, name="o4")
         b2_c = keep.tile([P, 4], F32, name="b2_c")
         b2_s = keep.tile([P, 4], F32, name="b2_s")
 
-        def bias2():
-            pb = psum.tile([P, 4, 4], F32, name="pb", tag="x")
+        def b2_mm():
+            pb = M["pb"] = psum.tile([P, 4, 4], F32, name="pb", tag="a")
             for c in range(4):
-                nc.tensor.matmul(pb[:, c, :], lhsT=b2_t[:, P * c:P * (c + 1)], rhs=pick[:], start=True, stop=True)
-            nc.vector.tensor_copy(out=b2_c[:], in_=pb[:, :, 0])
-            nc.vector.tensor_scalar(out=b2_s[:], in0=pb[:, :, 0], scalar1=SLOPE, scalar2=None, op0=ALU.mult)
+                pe.matmul(pb[:, c, :], lhsT=b2_t[:, P * c:P * (c + 1)], rhs=pick[:], start=True, stop=True)
 
-        def turned_mm(g, c):
-            acc = psum.tile([P, G], F32, name="acct", tag="x")
-            nc.tensor.matmul_mx(
-                out=acc[:], lhsT=w2_q[:, P * c:P * (c + 1)].bitcast(FP8X4), lhsT_scale=w2_s[:, P * c:P * (c + 1)],
-                rhs=hidden_q[g][:].bitcast(FP8X4), rhs_scale=hidden_s[g][:], start=True, stop=True)
-            return acc
+        def b2_out():
+            sca.copy(out=b2_c[:], in_=M["pb"][:, :, 0])
+            sca.activation(out=b2_s[:], in_=M["pb"][:, :, 0], func=ACT.Copy, scale=SLOPE)
+        S["b2m"] = b2_mm
+        S["b2o"] = b2_out
 
-        def turned_low(c, acc):
-            low = work.tile([P, G], F32, name="low", tag="low", bufs=8)
-            nc.scalar.activation(out=low[:], in_=acc[:], func=ACT.Identity, scale=SLOPE, bias=b2_s[:, c:c + 1])
-            return low
+        def put(tile):
+            nc.sync.dma_start(out=out_v[:, tile, :], in_=o4[:, tile, :])
 
-        def turned_max(c, acc, low):
-            ot = work.tile([P, G], F32, name="ot", tag="ot", bufs=8)
-            nc.vector.scalar_tensor_tensor(out=ot[:], in0=acc[:], scalar=b2_c[:, c:c + 1], in1=low[:], op0=ALU.add, op1=ALU.max)
-            return ot
+        def tm_step(L, c):
+            a, n = LG[L]
+            if n == G:
+                acc = M["ta", L, c] = psum.tile([P, G], F32, name="acct", tag="x")
+            else:
+                if ("tas", L, c // 2) not in M:
+                    M["tas", L, c // 2] = psum.tile([P, 2, n], F32, name="tas", tag="x")
+                acc = M["ta", L, c] = M["tas", L, c // 2][:, c % 2, :]
+            pe.matmul_mx(
+                out=acc[:, :], lhsT=w2_q[:, P * c:P * (c + 1)].bitcast(FP8X4), lhsT_scale=w2_s[:, P * c:P * (c + 1)],
+                rhs=hidden_q[:, a:a + n].bitcast(FP8X4), rhs_scale=hidden_s[:, a:a + n], start=True, stop=True)
 
-        def turned_back(c, ot, o4, copy):
-            back = psum.tile([P, 4, P], F32, name="back", tag="a")
-            for i in range(4):
-                nc.tensor.transpose(back[:, i, :], ot[:, P * i:P * (i + 1)], ident_f[:])
-            copy(out=o4[:, :, P * c:P * (c + 1)], in_=back[:])
+        def tl_step(L, c):
+            low = M["low", L, c] = work.tile([P, G], F32, name="low", tag="low", bufs=5)
+            sca.activation(out=low[:, 0:LG[L][1]], in_=M["ta", L, c][:, :], func=ACT.Identity, scale=SLOPE, bias=b2_s[:, c:c + 1])
 
-        nc.scalar.activation(out=warm2[:], in_=warm[:], func=ACT.Sin)
-        pick = keep.tile([P, 4], BF16, name="pick")
-        nc.vector.tensor_copy(out=pick[:, 0:2], in_=ident[:, 0:2])
-        nc.vector.tensor_copy(out=pick[:, 2:4], in_=ident[:, 32:34])
-        vcopy, scopy = nc.vector.tensor_copy, nc.scalar.copy
+        def tx_step(L, c):
+            n = LG[L][1]
+            top = M["top", L, c] = work.tile([P, G], F32, name="top", tag="top", bufs=6)
+            vec.scalar_tensor_tensor(out=top[:, 0:n], in0=M["ta", L, c][:, :], scalar=b2_c[:, c:c + 1], in1=M["low", L, c][:, 0:n], op0=ALU.add, op1=ALU.max)
 
-        ln = keep.tile([P, 9, P], BF16, name="ln")
-        for i, xt in enumerate((xt_t, xt_ws, xt_wd)):
-            nc.vector.tensor_copy(out=ln[:, :, 32 * (i + 1):32 * (i + 2)], in_=xt[:, 0:9].unsqueeze(2).to_broadcast([P, 9, 32]))
-            nc.vector.tensor_copy(out=ln[:, 3 * i:3 * i + 3, 0:32], in_=xt[:, 9:12].unsqueeze(2).to_broadcast([P, 3, 32]))
-        for n in range(9):
-            nc.tensor.transpose(xn[n // 6][:, n % 6, :], ln[:, n, :], ident[:])
-        w1_lay(1, vcopy)
+        def tb_step(L, i):
+            back = M["back", L, i] = psum.tile([P, C], F32, name="back", tag="a")
+            for c in range(4):
+                pe.transpose(back[:, P * c:P * (c + 1)], M["top", L, c][:, P * i:P * (i + 1)], ident_f[:])
 
-        pw = psum.tile([P, 16, 4], F32, name="pw", tag="x")
-        for t in range(4):
-            nc.tensor.matmul(pw[:, t, :], lhsT=rows_n[:, t:512:4], rhs=pick[:], start=True, stop=True)
-        for i in range(3):
-            for t in range(4):
-                at = 128 * (i + 1)
-                nc.tensor.matmul(pw[:, 4 + 4 * i + t, :], lhsT=rows_n[:, at + t:at + 512:4], rhs=pick[:], start=True, stop=True)
-        l0 = keep.tile([P, NT, P], BF16, name="l0")
-        nc.scalar.copy(out=l0[:, :, 80:120], in_=xt_d[:, :, 0].unsqueeze(2).to_broadcast([P, NT, 40]))
-        nc.scalar.copy(out=l0[:, :, 120:128], in_=xt_d[:, :, 1].unsqueeze(2).to_broadcast([P, NT, 8]))
-        nc.scalar.copy(out=wb_n[:], in_=pw[:, 0:4, 0:2].unsqueeze(1).to_broadcast([P, 3, 4, 2]))
-        nc.scalar.copy(out=wb_n[0:32], in_=pw[0:32, 4:16, 0:2].rearrange("p (i t) c -> p i t c", i=3))
-        v = [number_pre(0)]
-        w1_quant(1)
+        def to_step(L, i):
+            tile = LG[L][0] // P + i
+            sca.copy(out=o4[:, tile, :], in_=M["back", L, i][:])
+            put(tile)
 
-        lf = keep.tile([P, 3, P], BF16, name="lf")
-        nc.vector.tensor_copy(
-            out=lf[:].rearrange("p i (q j) -> p i q j", q=4),
-            in_=xt_d[:, :, 1].rearrange("p (q i) -> p i q", q=4).unsqueeze(3).to_broadcast([P, 3, 4, 32]))
-        for n in range(3):
-            nc.tensor.transpose(xn[1][:, 3 + n, :], lf[:, n, :], ident[:])
-        nc.vector.tensor_copy(
-            out=l0[:, :, 0:80].rearrange("p n (c j) -> p n c j", c=2),
-            in_=xt_s[:].unsqueeze(3).to_broadcast([P, NT, 2, 40]))
-        for n in range(NT):
-            nc.tensor.transpose(x0[n // 8][:, n % 8, :], l0[:, n, :], ident[:])
-        v.append(number_pre(1))
+        def nm_step(L, i):
+            a = LG[L][0] + P * i
+            acc = M["na", L, i] = psum.tile([P, C], F32, name="acc2", tag="x")
+            pe.matmul_mx(
+                out=acc[:], lhsT=hidden_q[:, a:a + P].bitcast(FP8X4), lhsT_scale=hidden_s[:, a:a + P],
+                rhs=w2_q[:].bitcast(FP8X4), rhs_scale=w2_s[:], start=True, stop=True)
 
-        fold_rows = keep.tile([P, 4, P], BF16, name="fold_rows")
-        fr = fold_rows[:].rearrange("p q j -> p (q j)")
+        def na_step(L, i):
+            v2 = M["v2", L, i] = work.tile([P, C], F32, name="v2", tag="v2", bufs=4)
+            vec.tensor_tensor(out=v2[:], in0=M["na", L, i][:], in1=b2_t[:], op=ALU.add)
 
-        def sine_weights(lhs, w0):
-            ps = psum.tile([P, 4, 4], F32, name="ps", tag="x")
-            for t in range(4):
-                nc.tensor.matmul(ps[:, t, :], lhsT=lhs[:, t:512:4], rhs=pick[:], start=True, stop=True)
-            o = slice(w0, w0 + 4)
-            nc.vector.tensor_copy(out=c_s[:, o], in_=ps[:, :, 2])
-            nc.vector.tensor_scalar(out=w_s[:, o], in0=ps[:, :, 0], scalar1=1.0 / TURN, scalar2=None, op0=ALU.mult)
-            nc.vector.scalar_tensor_tensor(out=b_s[:, o], in0=ps[:, :, 1], scalar=1.0 / TURN, in1=c_s[:, o], op0=ALU.mult, op1=ALU.add)
+        def no_step(L, i):
+            v2 = M["v2", L, i]
+            tile = LG[L][0] // P + i
+            vec.scalar_tensor_tensor(out=o4[:, tile, :], in0=v2[:], scalar=SLOPE, in1=v2[:], op0=ALU.mult, op1=ALU.max)
+            put(tile)
 
-        nc.vector.tensor_copy(out=fold_rows[:], in_=rows_s[:, 512:640].unsqueeze(1).to_broadcast([P, 4, P]))
-        w2_widen()
-        sine_weights(fr, 0)
-        number_relu(0, v[0])
-        yf = turns(xn[1][:, 3:6, :].rearrange("p n k -> p (n k)"), FOLD, 0)
-        number_relu(1, v[1])
-        w1_lay(0, scopy)
-        sine_weights(rows_s, 4)
-        ff = fraction(yf, FOLD)
-        y0 = turns(x0_of(0), G, 4)
-        v.append(number_pre(2))
-        w2_lay()
-        sine(fold[:], ff, FOLD)
-        f0 = fraction(y0, G)
-        number_relu(2, v[2])
-        for q in range(4):
-            nc.sync.dma_start(out=feat[1][0:32, FOLD * q:FOLD * (q + 1), :], in_=fold[32 * q:32 * q + 32, :, :])
-        w1_quant(0)
-        y1 = turns(x0_of(1), G, 4)
-        sine(feat0(0), f0, G)
-        w2_quant()
-        f1 = fraction(y1, G)
-        y2 = turns(x0_of(2), G, 4)
-        quant(1, 0)
-        quant(0, 0)
-        a0 = layer1(0)
-        sine(feat0(1), f1, G)
-        f2 = fraction(y2, G)
-        v10 = bias1(a0)
-        bias2()
-        quant(1, 1)
-        quant(0, 1)
-        a1 = layer1(1)
-        sine(feat0(2), f2, G)
-        h0 = relu1(0, v10)
-        v11 = bias1(a1)
-        quant(1, 2)
-        quant_h(0, h0)
-        quant(0, 2)
-        o4 = [work.tile([P, 4, C], F32, name="o4_%d" % g, tag="o4", bufs=3) for g in range(NG)]
+        for g in ("F", 0, 1, 2):
+            S["y%s" % g] = lambda g=g: y_step(g)
+            S["k%s" % g] = lambda g=g: k_step(g)
+            S["f%s" % g] = lambda g=g: f_step(g)
+        S["sF"] = lambda: sin_step("F")
+        for L in range(len(LG)):
+            S["s%d" % L] = lambda L=L: sin_step(L)
+            S["q1%d" % L] = lambda L=L: q_step(1, L)
+            S["q0%d" % L] = lambda L=L: q_step(0, L)
+            S["h%d" % L] = lambda L=L: h_step(L)
+            S["qh%d" % L] = lambda L=L: qh_step(L)
+            for c in range(4):
+                S["m%d%d" % (L, c)] = lambda L=L, c=c: m1_step(L, c)
+                S["v%d%d" % (L, c)] = lambda L=L, c=c: v1_step(L, c)
+                if L in TURNED:
+                    S["tm%d%d" % (L, c)] = lambda L=L, c=c: tm_step(L, c)
+                    S["tl%d%d" % (L, c)] = lambda L=L, c=c: tl_step(L, c)
+                    S["tx%d%d" % (L, c)] = lambda L=L, c=c: tx_step(L, c)
+            for i in range(LG[L][1] // P):
+                if L in TURNED:
+                    S["tb%d%d" % (L, i)] = lambda L=L, i=i: tb_step(L, i)
+                    S["to%d%d" % (L, i)] = lambda L=L, i=i: to_step(L, i)
+                else:
+                    S["nm%d%d" % (L, i)] = lambda L=L, i=i: nm_step(L, i)
+                    S["na%d%d" % (L, i)] = lambda L=L, i=i: na_step(L, i)
+                    S["no%d%d" % (L, i)] = lambda L=L, i=i: no_step(L, i)
 
-        ac = [[None] * 4 for g in range(NG)]
-        lo = [[None] * 4 for g in range(NG)]
-        ot = [[None] * 4 for g in range(NG)]
-
-        def mm(g, c):
-            ac[g][c] = turned_mm(g, c)
-
-        def low(g, c):
-            lo[g][c] = turned_low(c, ac[g][c])
-
-        def top(g, c):
-            ot[g][c] = turned_max(c, ac[g][c], lo[g][c])
-
-        def back(g, c, copy):
-            turned_back(c, ot[g][c], o4[g], copy)
-            nc.sync.dma_start(out=out_v[:, 4 * g:4 * g + 4, P * c:P * (c + 1)], in_=o4[g][:, :, P * c:P * (c + 1)])
-
-        for c in range(4):
-            mm(0, c)
-        a2 = layer1(2)
-        h1 = relu1(1, v11)
-        for c in range(4):
-            low(0, c)
-        v12 = bias1(a2)
-        units = [(g, c) for g in range(NG) for c in range(4)]
-        for s, u in enumerate(units):
-            if s == 3:
-                h2 = relu1(2, v12)
-            top(*u)
-            if s == 0:
-                quant_h(1, h1)
-            if s == 3:
-                quant_h(2, h2)
-            if s + 4 < len(units):
-                mm(*units[s + 4])
-                low(*units[s + 4])
-            if s >= 2:
-                back(*units[s - 2], vcopy if s - 2 in V_BACK else scopy)
-        back(*units[-2], vcopy)
-        back(*units[-1], scopy)
+        sca.activation(out=warm2[:], in_=warm[:], func=ACT.Sin)
+        for name in ORDER.split():
+            S[name]()

@@ -25,11 +25,14 @@ FOLD = 384
 SLOPE = 0.01
 TURN = 2.0 * math.pi
 
-TURNED = (0, 1,)
-LG = ((0, 512), (512, 512), (1024, 512))
+TURNED = (0, 1)
+SUMMED = ()
+SHIFTED = ()
+SHIFT = 4096.0
+LG = ((0, 512), (512, 512), (1024, 256), (1280, 256))
 
 ORDER = """
-pick ln w2wid0 w1lay1 xn pw l0 wbn w1q1 w2wid2 frow smF b2m lf nv1 sm0 w1lay0 spF soF nr1 nv0 yF nr0 sp0 so0 w2wid3 kF y0 fF nv2 k0 y1 sF f0 nr2 k1 w1q0 s0 y2 f1 sd s1 q00 q10 b2o k2 m01 m00 q11 v00 v01 f2 m03 w2wid1 q01 m02 w2lay v02 v03 m11 h0 w2q s2 m12 qh0 v11 m10 m13 q12 tm01 tm03 v12 q02 tm00 v13 m21 v10 m22 tl03 tl00 v21 h1 tl01 m23 tm02 v22 tx03 tx01 m20 v23 tl02 qh1 tm10 v20 tm12 tx00 tx02 tl12 h2 tl10 tm13 tm11 tb01 tb00 to01 tb03 tx10 tb02 to00 tl11 qh2 tx12 nm21 tl13 nm22 to03 tx11 tx13 tb13 to02 na21 to13 tb10 na22 to10 nm23 tb12 nm20 no21 tb11 to12 na23 no22 na20 to11 no23 no20
+w1lay1 b2d pw ln w1q1 xn lf wbn nv0 frow smF spF sm0 l0 nv1 w1lay0 soF nr0 yF sp0 w1q0 kF so0 nv2 nr1 y0 y1 fF sF nr2 w2wid1 k0 y2 k1 f0 s0 f1 b2m sd q10 q00 k2 w2wid2 q11 q12 b2o w2wid0 s1 m02 f2 v02 m01 q01 m00 w2wid3 v01 v00 m03 v03 s2 m10 q13 m12 m11 m13 w2lay v10 v12 s3 h0 q02 m20 m21 v11 v13 v20 m22 v22 v21 w2q m23 v23 qh0 q03 tm01 tl01 h1 tm03 tx01 tl03 tx03 qh1 tm00 tl00 tx00 m33 tm02 v33 tl02 m30 v30 m32 v32 m31 v31 tm10 tm12 tl10 tx02 h2 tl12 tb00 to00 tm11 tm13 tl11 tx10 qh2 tl13 tb02 to02 h3 tb03 to03 tb01 nm21 tx12 to01 nm20 tx11 tx13 tb11 na20 tb12 to11 to12 tb10 qh3 nm31 na21 nm30 no20 no21 to10 tb13 na31 to13 na30 no31 no30
 """
 
 FLOPS = 2 * B * (FEAT * C + C * C)
@@ -51,11 +54,15 @@ def tile_claimencoder_kernel(
 
         rows_n = keep.tile([P, 896], BF16, name="rows_n")
         nc.vector.memset(rows_n[:], 0.0)
+        pick = keep.tile([P, 4], BF16, name="pick")
+        nc.vector.memset(pick[:], 0.0)
+        for c, q in enumerate((0, 64, 32)):
+            nc.vector.memset(pick[q:q + 1, c:c + 1], 1.0)
         rows_s = keep.tile([P, 640], BF16, name="rows_s")
         nc.vector.memset(rows_s[:], 0.0)
         nc.vector.memset(rows_s[32:33, :].rearrange("p (g h j) -> p g h j", g=4, h=2)[:, :, 1, :], 0.25)
         ident = keep.tile([P, P], BF16, name="ident")
-        make_identity(nc, ident[:])
+        ident_f = keep.tile([P, P], F32, name="ident_f")
         warm = keep.tile([P, 1], F32, name="warm")
         nc.gpsimd.memset(warm[:], 0.0)
         warm2 = keep.tile([P, 1], F32, name="warm2")
@@ -74,29 +81,39 @@ def tile_claimencoder_kernel(
             queue.dma_start(out=rows[r:r + 1, at:at + n], in_=vec.rearrange("(o n) -> o n", o=1))
 
         w1v = W1.rearrange("(g p t) c -> g p t c", g=2, t=4)
-        for i, vec in enumerate((time_s, wait_src, wait_dst)):
-            nc.sync.dma_start(out=xt_n[:, i, 0:NT], in_=vec.rearrange("(p n) -> p n", n=NT))
         row(nc.scalar, rows_n, t_w, 0, 128)
-        row(nc.scalar, rows_n, t_b, 1, 128)
+        row(nc.scalar, rows_n, t_b, 64, 128)
         row(nc.scalar, rows_n, ws_w, 0, 256)
-        row(nc.scalar, rows_n, ws_b, 1, 256)
+        row(nc.scalar, rows_n, ws_b, 64, 256)
+        row(nc.scalar, rows_n, wd_w, 0, 384)
+        row(nc.scalar, rows_n, wd_b, 64, 384)
+        nc.sync.dma_start(out=xt_n[:, 0, 0:NT], in_=time_s.rearrange("(p n) -> p n", n=NT))
         nc.sync.dma_start(out=w1_raw[1][:], in_=w1v[1])
-        row(nc.sync, rows_n, wd_w, 0, 384)
-        row(nc.sync, rows_n, wd_b, 1, 384)
+        nc.gpsimd.dma_start(out=xt_n[:, 1, 0:NT], in_=wait_src.rearrange("(p n) -> p n", n=NT))
+        nc.gpsimd.dma_start(out=xt_n[:, 2, 0:NT], in_=wait_dst.rearrange("(p n) -> p n", n=NT))
+        make_identity(nc, ident[:])
+        nc.sync.dma_start(out=xt_d[:].rearrange("p n c -> p (n c)"), in_=dst_xy.rearrange("(p n) c -> p (n c)", n=NT))
+        row(nc.sync, rows_s, dst_wsy, 0, 480)
+        row(nc.sync, rows_s, dst_bsy, 64, 480)
+        row(nc.sync, rows_s, dst_wcy, 0, 560)
+        row(nc.sync, rows_s, dst_bcy, 64, 560)
+        nc.sync.dma_start(out=xt_s[:].rearrange("p n c -> p (n c)"), in_=src_xy.rearrange("(p n) c -> p (n c)", n=NT))
+        row(nc.sync, rows_s, src_wsx, 0, 0)
+        row(nc.sync, rows_s, src_bsx, 64, 0)
+        row(nc.sync, rows_s, src_wcx, 0, 80)
+        row(nc.sync, rows_s, src_bcx, 64, 80)
+        row(nc.sync, rows_s, src_wsy, 0, 160)
+        row(nc.sync, rows_s, src_bsy, 64, 160)
+        row(nc.sync, rows_s, src_wcy, 0, 240)
+        row(nc.sync, rows_s, src_bcy, 64, 240)
+        row(nc.sync, rows_s, dst_wsx, 0, 320)
+        row(nc.sync, rows_s, dst_bsx, 64, 320)
+        nc.gpsimd.dma_start(out=w1_raw[0][:], in_=w1v[0])
+        row(nc.gpsimd, rows_s, dst_wcx, 0, 400)
+        row(nc.gpsimd, rows_s, dst_bcx, 64, 400)
+        nc.gpsimd.dma_start(out=b1_t[:], in_=b1.rearrange("(p t) -> p t", t=4))
         nc.sync.dma_start(out=w2_scl[:], in_=W2_scale.rearrange("(p t) o -> p (t o)", t=4))
         nc.sync.dma_start(out=w2_raw[:], in_=W2_bytes.rearrange("(p t) c -> p t c", t=4))
-        nc.sync.dma_start(out=xt_d[:].rearrange("p n c -> p (n c)"), in_=dst_xy.rearrange("(p n) c -> p (n c)", n=NT))
-        nc.sync.dma_start(out=xt_s[:].rearrange("p n c -> p (n c)"), in_=src_xy.rearrange("(p n) c -> p (n c)", n=NT))
-        nc.sync.dma_start(out=w1_raw[0][:], in_=w1v[0])
-        for i, (w, b) in enumerate(((dst_wsy, dst_bsy), (dst_wcy, dst_bcy))):
-            row(nc.sync, rows_s, w, 0, 480 + 80 * i)
-            row(nc.sync, rows_s, b, 1, 480 + 80 * i)
-        for i, (w, b) in enumerate(((src_wsx, src_bsx), (src_wcx, src_bcx), (src_wsy, src_bsy), (src_wcy, src_bcy), (dst_wsx, dst_bsx), (dst_wcx, dst_bcx))):
-            row(nc.sync, rows_s, w, 0, 80 * i)
-            row(nc.sync, rows_s, b, 1, 80 * i)
-        nc.gpsimd.dma_start(out=b1_t[:], in_=b1.rearrange("(p t) -> p t", t=4))
-        nc.gpsimd.dma_start(out=b2_t[:], in_=b2.partition_broadcast(P))
-        ident_f = keep.tile([P, P], F32, name="ident_f")
         make_identity(nc, ident_f[:])
 
         vec, sca, pe = nc.vector, nc.scalar, nc.tensor
@@ -133,18 +150,12 @@ def tile_claimencoder_kernel(
         w_s = keep.tile([P, 8], F32, name="w_s")
         b_s = keep.tile([P, 8], F32, name="b_s")
         c_s = keep.tile([P, 8], F32, name="c_s")
-        pick = keep.tile([P, 4], BF16, name="pick")
         ln = keep.tile([P, 9, P], BF16, name="ln")
         lf = keep.tile([P, 3, P], BF16, name="lf")
         l0 = keep.tile([P, NT, P], BF16, name="l0")
         fold_rows = keep.tile([P, 4, P], BF16, name="fold_rows")
         fr = fold_rows[:].rearrange("p q j -> p (q j)")
         M = {}
-
-        def pick_step():
-            nc.gpsimd.tensor_copy(out=pick[:, 0:2], in_=ident[:, 0:2])
-            nc.gpsimd.tensor_copy(out=pick[:, 2:4], in_=ident[:, 32:34])
-        S["pick"] = pick_step
 
         def ln_step():
             vec.tensor_copy(
@@ -260,7 +271,7 @@ def tile_claimencoder_kernel(
                 a, n = LG[L]
                 dst, src = feat[0][:, a:a + n, :], M["y", a // G][:, :, a % G:a % G + n]
             sca.activation(
-                out=dst.rearrange("p (c i) t -> p c t i", i=4), in_=src.rearrange("p t (c i) -> p c t i", i=4), func=ACT.Sin, scale=TURN)
+                out=dst.rearrange("p (c i) t -> p c t i", i=2), in_=src.rearrange("p t (c i) -> p c t i", i=2), func=ACT.Sin, scale=TURN)
 
         def move_step():
             for q in range(4):
@@ -319,6 +330,7 @@ def tile_claimencoder_kernel(
         def b2_out():
             sca.copy(out=b2_c[:], in_=M["pb"][:, :, 0])
             sca.activation(out=b2_s[:], in_=M["pb"][:, :, 0], func=ACT.Copy, scale=SLOPE)
+        S["b2d"] = lambda: nc.sync.dma_start(out=b2_t[:], in_=b2.partition_broadcast(P))
         S["b2m"] = b2_mm
         S["b2o"] = b2_out
 

import math
from contextlib import ExitStack

import concourse.mybir as mybir
from concourse.masks import make_identity

F32 = mybir.dt.float32
BF16 = mybir.dt.bfloat16
I32 = mybir.dt.int32
U32 = mybir.dt.uint32
U8 = mybir.dt.uint8
FP8 = mybir.dt.float8_e4m3fn
FP8X4 = mybir.dt.float8_e4m3fn_x4
ACT = mybir.ActivationFunctionType
ALU = mybir.AluOpType

P = 128
B = 1536
C = 512
FEAT = 1024
NT = B // P
G = 512
NG = B // G
FOLD = 384
SLOPE = 0.01
TURN = 2.0 * math.pi

TURNED = (0, 1)
SUMMED = ()
SHIFTED = ()
SHIFT = 4096.0
LG = ((0, 512), (512, 512), (1024, 256), (1280, 256))

ORDER = """
w1lay1 b2d pw ln w1q1 xn lf wbn nv0 frow smF spF sm0 l0 nv1 w1lay0 soF nr0 yF sp0 w1q0 kF so0 nv2 nr1 y0 y1 fF sF nr2 w2wid1 k0 y2 k1 f0 s0 f1 b2m sd q10 q00 k2 w2wid2 q11 q12 b2o w2wid0 s1 m02 f2 v02 m01 q01 m00 w2wid3 v01 v00 m03 v03 s2 m10 q13 m12 m11 m13 w2lay v10 v12 s3 h0 q02 m20 m21 v11 v13 v20 m22 v22 v21 w2q m23 v23 qh0 q03 tm01 tl01 h1 tm03 tx01 tl03 tx03 qh1 tm00 tl00 tx00 m33 tm02 v33 tl02 m30 v30 m32 v32 m31 v31 tm10 tm12 tl10 tx02 h2 tl12 tb00 to00 tm11 tm13 tl11 tx10 qh2 tl13 tb02 to02 h3 tb03 to03 tb01 nm21 tx12 to01 nm20 tx11 tx13 tb11 na20 tb12 to11 to12 tb10 qh3 nm31 na21 nm30 no20 no21 to10 tb13 na31 to13 na30 no31 no30
"""

FLOPS = 2 * B * (FEAT * C + C * C)


def tile_claimencoder_kernel(
    tc, src_xy, dst_xy, time_s, wait_src, wait_dst,
    src_wsx, src_bsx, src_wcx, src_bcx, src_wsy, src_bsy, src_wcy, src_bcy,
    dst_wsx, dst_bsx, dst_wcx, dst_bcx, dst_wsy, dst_bsy, dst_wcy, dst_bcy,
    t_w, t_b, ws_w, ws_b, wd_w, wd_b,
    W1, b1, W2_bytes, W2_scale, b2, out,
):
    nc = tc.nc
    with ExitStack() as ctx:
        keep = ctx.enter_context(tc.tile_pool(name="keep", bufs=1))
        work = ctx.enter_context(tc.tile_pool(name="work", bufs=2))
        psum = ctx.enter_context(tc.psum_pool(name="psum", bufs=4))
        ctx.enter_context(tc.manual_schedule())

        rows_n = keep.tile([P, 896], BF16, name="rows_n")
        nc.vector.memset(rows_n[:], 0.0)
        pick = keep.tile([P, 4], BF16, name="pick")
        nc.vector.memset(pick[:], 0.0)
        for c, q in enumerate((0, 64, 32)):
            nc.vector.memset(pick[q:q + 1, c:c + 1], 1.0)
        rows_s = keep.tile([P, 640], BF16, name="rows_s")
        nc.vector.memset(rows_s[:], 0.0)
        nc.vector.memset(rows_s[32:33, :].rearrange("p (g h j) -> p g h j", g=4, h=2)[:, :, 1, :], 0.25)
        ident = keep.tile([P, P], BF16, name="ident")
        ident_f = keep.tile([P, P], F32, name="ident_f")
        warm = keep.tile([P, 1], F32, name="warm")
        nc.gpsimd.memset(warm[:], 0.0)
        warm2 = keep.tile([P, 1], F32, name="warm2")

        xt_n = keep.tile([P, 3, 16], BF16, name="xt_n")
        xt_s = keep.tile([P, NT, 2], BF16, name="xt_s")
        xt_d = keep.tile([P, NT, 2], BF16, name="xt_d")
        w1_raw = [keep.tile([P, 4, C], BF16, name="w1_raw%d" % i) for i in range(2)]
        w2_raw = keep.tile([P, 4, C], U8, name="w2_raw")
        w2_scl = keep.tile([P, 4], F32, name="w2_scl")
        b1_t = keep.tile([P, 4], BF16, name="b1_t")
        b2_t = keep.tile([P, C], BF16, name="b2_t")

        def row(queue, rows, vec, r, at):
            n = vec.shape[0]
            queue.dma_start(out=rows[r:r + 1, at:at + n], in_=vec.rearrange("(o n) -> o n", o=1))

        w1v = W1.rearrange("(g p t) c -> g p t c", g=2, t=4)
        row(nc.scalar, rows_n, t_w, 0, 128)
        row(nc.scalar, rows_n, t_b, 64, 128)
        row(nc.scalar, rows_n, ws_w, 0, 256)
        row(nc.scalar, rows_n, ws_b, 64, 256)
        row(nc.scalar, rows_n, wd_w, 0, 384)
        row(nc.scalar, rows_n, wd_b, 64, 384)
        nc.sync.dma_start(out=xt_n[:, 0, 0:NT], in_=time_s.rearrange("(p n) -> p n", n=NT))
        nc.sync.dma_start(out=w1_raw[1][:], in_=w1v[1])
        nc.gpsimd.dma_start(out=xt_n[:, 1, 0:NT], in_=wait_src.rearrange("(p n) -> p n", n=NT))
        nc.gpsimd.dma_start(out=xt_n[:, 2, 0:NT], in_=wait_dst.rearrange("(p n) -> p n", n=NT))
        make_identity(nc, ident[:])
        nc.sync.dma_start(out=xt_d[:].rearrange("p n c -> p (n c)"), in_=dst_xy.rearrange("(p n) c -> p (n c)", n=NT))
        row(nc.sync, rows_s, dst_wsy, 0, 480)
        row(nc.sync, rows_s, dst_bsy, 64, 480)
        row(nc.sync, rows_s, dst_wcy, 0, 560)
        row(nc.sync, rows_s, dst_bcy, 64, 560)
        nc.sync.dma_start(out=xt_s[:].rearrange("p n c -> p (n c)"), in_=src_xy.rearrange("(p n) c -> p (n c)", n=NT))
        row(nc.sync, rows_s, src_wsx, 0, 0)
        row(nc.sync, rows_s, src_bsx, 64, 0)
        row(nc.sync, rows_s, src_wcx, 0, 80)
        row(nc.sync, rows_s, src_bcx, 64, 80)
        row(nc.sync, rows_s, src_wsy, 0, 160)
        row(nc.sync, rows_s, src_bsy, 64, 160)
        row(nc.sync, rows_s, src_wcy, 0, 240)
        row(nc.sync, rows_s, src_bcy, 64, 240)
        row(nc.sync, rows_s, dst_wsx, 0, 320)
        row(nc.sync, rows_s, dst_bsx, 64, 320)
        nc.gpsimd.dma_start(out=w1_raw[0][:], in_=w1v[0])
        row(nc.gpsimd, rows_s, dst_wcx, 0, 400)
        row(nc.gpsimd, rows_s, dst_bcx, 64, 400)
        nc.gpsimd.dma_start(out=b1_t[:], in_=b1.rearrange("(p t) -> p t", t=4))
        nc.sync.dma_start(out=w2_scl[:], in_=W2_scale.rearrange("(p t) o -> p (t o)", t=4))
        nc.sync.dma_start(out=w2_raw[:], in_=W2_bytes.rearrange("(p t) c -> p t c", t=4))
        make_identity(nc, ident_f[:])

        vec, sca, pe = nc.vector, nc.scalar, nc.tensor
        S = {}

        w1_q = [keep.tile([P, C], U32, name="w1_q%d" % i, align_bytes=64) for i in range(2)]
        w1_s = [keep.tile([P, C], U8, name="w1_s%d" % i, align_bytes=64) for i in range(2)]
        w1_g = [keep.tile([P, C * 4], BF16, name="w1_g%d" % i, align_bytes=64) for i in range(2)]
        w2_q = keep.tile([P, C], U32, name="w2_q", align_bytes=64)
        w2_s = keep.tile([P, C], U8, name="w2_s", align_bytes=64)
        w2_b = keep.tile([P, 4, C], BF16, name="w2_b")
        w2_g = keep.tile([P, C, 4], BF16, name="w2_g", align_bytes=64)

        def w1_lay(i, copy):
            copy(out=w1_g[i][:].rearrange("p (t m j) -> p t m j", t=4, j=4), in_=w1_raw[i][:].rearrange("p j (m t) -> p t m j", t=4))

        S["w1lay1"] = lambda: w1_lay(1, vec.tensor_copy)
        S["w1lay0"] = lambda: w1_lay(0, vec.tensor_copy)
        for i in range(2):
            S["w1q%d" % i] = lambda i=i: vec.quantize_mx(out=w1_q[i][:].bitcast(FP8X4), scales=w1_s[i][:], in_=w1_g[i][:])

        def w2_widen(t):
            sca.activation(out=w2_b[:, t, :], in_=w2_raw[:, t, :].bitcast(FP8), func=ACT.Copy, scale=w2_scl[:, t:t + 1])
        for t in range(4):
            S["w2wid%d" % t] = lambda t=t: w2_widen(t)
        S["w2lay"] = lambda: vec.tensor_copy(out=w2_g[:].rearrange("p (c i) t -> p c t i", i=4), in_=w2_b[:].rearrange("p t (c i) -> p c t i", i=4))
        S["w2q"] = lambda: vec.quantize_mx(out=w2_q[:].bitcast(FP8X4), scales=w2_s[:], in_=w2_g[:].rearrange("p c t -> p (c t)"))

        feat = [keep.tile([P, B, 4], BF16, name="feat%d" % i, align_bytes=64) for i in range(2)]
        feat_q = [keep.tile([P, B], U32, name="feat_q%d" % i, align_bytes=64) for i in range(2)]
        feat_s = [keep.tile([P, B], U8, name="feat_s%d" % i, align_bytes=64) for i in range(2)]
        fold = keep.tile([P, FOLD, 4], BF16, name="fold")
        wb_n = keep.tile([P, 3, 4, 2], F32, name="wb_n")
        w_s = keep.tile([P, 8], F32, name="w_s")
        b_s = keep.tile([P, 8], F32, name="b_s")
        c_s = keep.tile([P, 8], F32, name="c_s")
        ln = keep.tile([P, 9, P], BF16, name="ln")
        lf = keep.tile([P, 3, P], BF16, name="lf")
        l0 = keep.tile([P, NT, P], BF16, name="l0")
        fold_rows = keep.tile([P, 4, P], BF16, name="fold_rows")
        fr = fold_rows[:].rearrange("p q j -> p (q j)")
        M = {}

        def ln_step():
            vec.tensor_copy(
                out=ln[:, :, 32:128].rearrange("p n (i j) -> p n i j", i=3),
                in_=xt_n[:, :, 0:9].rearrange("p i n -> p n i").unsqueeze(3).to_broadcast([P, 9, 3, 32]))
            vec.tensor_copy(
                out=ln[:, :, 0:32].rearrange("p (i n) j -> p i n j", i=3),
                in_=xt_n[:, :, 9:12].unsqueeze(3).to_broadcast([P, 3, 3, 32]))
        S["ln"] = ln_step

        def xn_step():
            M["xn"] = [psum.tile([P, 8, P], BF16, name="xn%d" % i, tag="a") for i in range(2)]
            for n in range(9):
                pe.transpose(M["xn"][n // 6][:, n % 6, :], ln[:, n, :], ident[:])
        S["xn"] = xn_step

        def lf_step():
            vec.tensor_copy(
                out=lf[:].rearrange("p i (q j) -> p i q j", q=4),
                in_=xt_d[:, :, 1].rearrange("p (q i) -> p i q", q=4).unsqueeze(3).to_broadcast([P, 3, 4, 32]))
            for n in range(3):
                pe.transpose(M["xn"][1][:, 3 + n, :], lf[:, n, :], ident[:])
        S["lf"] = lf_step

        def l0_step():
            vec.tensor_copy(out=l0[:, :, 80:120], in_=xt_d[:, :, 0].unsqueeze(2).to_broadcast([P, NT, 40]))
            vec.tensor_copy(out=l0[:, :, 120:128], in_=xt_d[:, :, 1].unsqueeze(2).to_broadcast([P, NT, 8]))
            vec.tensor_copy(
                out=l0[:, :, 0:80].rearrange("p n (c j) -> p n c j", c=2),
                in_=xt_s[:].unsqueeze(3).to_broadcast([P, NT, 2, 40]))
            M["x0"] = [psum.tile([P, 8, P], BF16, name="x0%d" % i, tag="x") for i in range(2)]
            for n in range(NT):
                pe.transpose(M["x0"][n // 8][:, n % 8, :], l0[:, n, :], ident[:])
        S["l0"] = l0_step

        def pw_step():
            pw = M["pw"] = psum.tile([P, 16, 4], F32, name="pw", tag="x")
            for t in range(4):
                pe.matmul(pw[:, t, :], lhsT=rows_n[:, t:512:4], rhs=pick[:], start=True, stop=True)
            for i in range(3):
                for t in range(4):
                    at = 128 * (i + 1)
                    pe.matmul(pw[:, 4 + 4 * i + t, :], lhsT=rows_n[:, at + t:at + 512:4], rhs=pick[:], start=True, stop=True)
        S["pw"] = pw_step

        def wbn_step():
            sca.copy(out=wb_n[:], in_=M["pw"][:, 0:4, 0:2].unsqueeze(1).to_broadcast([P, 3, 4, 2]))
            sca.copy(out=wb_n[0:32], in_=M["pw"][0:32, 4:16, 0:2].rearrange("p (i t) c -> p i t c", i=3))
        S["wbn"] = wbn_step

        def nv_step(i):
            v = M["v", i] = work.tile([P, 4, FOLD], F32, name="v", tag="v")
            src = M["xn"][i // 2][:, 3 * (i % 2):3 * (i % 2) + 3, :].rearrange("p n k -> p (n k)")
            for t in range(4):
                sca.activation(out=v[:, t, :], in_=src, func=ACT.Identity, scale=wb_n[:, i, t, 0:1], bias=wb_n[:, i, t, 1:2])

        def nr_step(i):
            vv = M["v", i][:].rearrange("p t n -> p n t")
            vec.scalar_tensor_tensor(out=feat[1][:, FOLD * i:FOLD * (i + 1), :], in0=vv, scalar=SLOPE, in1=vv, op0=ALU.mult, op1=ALU.max)
            nc.sync.dma_start(out=feat[1][32 * (i + 1):32 * (i + 2), 1152:1536, :], in_=feat[1][0:32, FOLD * i:FOLD * (i + 1), :])
        for i in range(3):
            S["nv%d" % i] = lambda i=i: nv_step(i)
            S["nr%d" % i] = lambda i=i: nr_step(i)

        S["frow"] = lambda: vec.tensor_copy(out=fold_rows[:], in_=rows_s[:, 512:640].unsqueeze(1).to_broadcast([P, 4, P]))

        def sw_mm(w0, lhs):
            ps = M["ps", w0] = psum.tile([P, 4, 4], F32, name="ps", tag="x")
            for t in range(4):
                pe.matmul(ps[:, t, :], lhsT=lhs[:, t:512:4], rhs=pick[:], start=True, stop=True)

        def sw_part(w0):
            ps = M["ps", w0]
            o = slice(w0, w0 + 4)
            sca.copy(out=c_s[:, o], in_=ps[:, :, 2])
            sca.activation(out=w_s[:, o], in_=ps[:, :, 0], func=ACT.Copy, scale=1.0 / TURN)

        def sw_out(w0):
            ps = M["ps", w0]
            o = slice(w0, w0 + 4)
            vec.scalar_tensor_tensor(out=b_s[:, o], in0=ps[:, :, 1], scalar=1.0 / TURN, in1=c_s[:, o], op0=ALU.mult, op1=ALU.add)
        S["smF"] = lambda: sw_mm(0, fr)
        S["sm0"] = lambda: sw_mm(4, rows_s)
        S["spF"] = lambda: sw_part(0)
        S["sp0"] = lambda: sw_part(4)
        S["soF"] = lambda: sw_out(0)
        S["so0"] = lambda: sw_out(4)

        def y_step(g):
            n, w0 = (FOLD, 0) if g == "F" else (G, 4)
            if g == "F":
                x = M["xn"][1][:, 3:6, :]
            else:
                x = M["x0"][g // 2][:, 4 * (g % 2):4 * (g % 2) + 4, :]
            y = M["y", g] = work.tile([P, 4, G], F32, name="y", tag="y", bufs=3)
            for t in range(4):
                sca.activation(out=y[:, t, 0:n], in_=x.rearrange("p n k -> p (n k)"), func=ACT.Identity, scale=w_s[:, w0 + t:w0 + t + 1], bias=b_s[:, w0 + t:w0 + t + 1])

        def k_step(g):
            n = FOLD if g == "F" else G
            k = M["k", g] = work.tile([P, 4, G], I32, name="k", tag="k")
            vec.tensor_copy(out=k[:, :, 0:n], in_=M["y", g][:, :, 0:n])

        def f_step(g):
            n = FOLD if g == "F" else G
            y, k = M["y", g], M["k", g]
            vec.tensor_tensor(out=y[:, :, 0:n], in0=y[:, :, 0:n], in1=k[:, :, 0:n], op=ALU.subtract)

        def sin_step(L):
            if L == "F":
                dst, src = fold[:], M["y", "F"][:, :, 0:FOLD]
            else:
                a, n = LG[L]
                dst, src = feat[0][:, a:a + n, :], M["y", a // G][:, :, a % G:a % G + n]
            sca.activation(
                out=dst.rearrange("p (c i) t -> p c t i", i=2), in_=src.rearrange("p t (c i) -> p c t i", i=2), func=ACT.Sin, scale=TURN)

        def move_step():
            for q in range(4):
                nc.sync.dma_start(out=feat[1][0:32, FOLD * q:FOLD * (q + 1), :], in_=fold[32 * q:32 * q + 32, :, :])
        S["sd"] = move_step

        def q_step(i, L):
            s = slice(LG[L][0], LG[L][0] + LG[L][1])
            vec.quantize_mx(
                out=feat_q[i][:, s].bitcast(FP8X4), scales=feat_s[i][:, s],
                in_=feat[i][:, s, :].rearrange("p n t -> p (n t)"))

        def m1_step(L, t):
            a, n = LG[L]
            s = slice(a, a + n)
            if n == G:
                acc = M["acc", L, t] = psum.tile([P, G], F32, name="acc", tag="a")
            else:
                if ("accs", L, t // 2) not in M:
                    M["accs", L, t // 2] = psum.tile([P, 2, n], F32, name="accs", tag="a")
                acc = M["acc", L, t] = M["accs", L, t // 2][:, t % 2, :]
            for i in range(2):
                pe.matmul_mx(
                    out=acc[:, :], lhsT=w1_q[i][:, P * t:P * (t + 1)].bitcast(FP8X4), lhsT_scale=w1_s[i][:, P * t:P * (t + 1)],
                    rhs=feat_q[i][:, s].bitcast(FP8X4), rhs_scale=feat_s[i][:, s], start=(i == 0), stop=(i == 1))

        def v1_step(L, t):
            if ("v1", L) not in M:
                M["v1", L] = work.tile([P, 4, G], F32, name="v1", tag="v1", bufs=3)
            n = LG[L][1]
            sca.activation(out=M["v1", L][:, t, 0:n], in_=M["acc", L, t][:, :], func=ACT.Identity, bias=b1_t[:, t:t + 1])

        def h_step(L):
            n = LG[L][1]
            h = M["h", L] = work.tile([P, G, 4], BF16, name="h", tag="h", align_bytes=64)
            vv = M["v1", L][:, :, 0:n].rearrange("p t n -> p n t")
            vec.scalar_tensor_tensor(out=h[:, 0:n, :], in0=vv, scalar=SLOPE, in1=vv, op0=ALU.mult, op1=ALU.max)

        hidden_q = keep.tile([P, B], U32, name="hidden_q", align_bytes=64)
        hidden_s = keep.tile([P, B], U8, name="hidden_s", align_bytes=64)

        def qh_step(L):
            a, n = LG[L]
            vec.quantize_mx(out=hidden_q[:, a:a + n].bitcast(FP8X4), scales=hidden_s[:, a:a + n], in_=M["h", L][:, 0:n, :].rearrange("p n t -> p (n t)"))

        out_v = out.rearrange("(p n) c -> p n c", n=NT)
        o4 = keep.tile([P, NT, C], F32, name="o4")
        b2_c = keep.tile([P, 4], F32, name="b2_c")
        b2_s = keep.tile([P, 4], F32, name="b2_s")

        def b2_mm():
            pb = M["pb"] = psum.tile([P, 4, 4], F32, name="pb", tag="a")
            for c in range(4):
                pe.matmul(pb[:, c, :], lhsT=b2_t[:, P * c:P * (c + 1)], rhs=pick[:], start=True, stop=True)

        def b2_out():
            sca.copy(out=b2_c[:], in_=M["pb"][:, :, 0])
            sca.activation(out=b2_s[:], in_=M["pb"][:, :, 0], func=ACT.Copy, scale=SLOPE)
        S["b2d"] = lambda: nc.sync.dma_start(out=b2_t[:], in_=b2.partition_broadcast(P))
        S["b2m"] = b2_mm
        S["b2o"] = b2_out

        def put(tile):
            nc.sync.dma_start(out=out_v[:, tile, :], in_=o4[:, tile, :])

        def tm_step(L, c):
            a, n = LG[L]
            if n == G:
                acc = M["ta", L, c] = psum.tile([P, G], F32, name="acct", tag="x")
            else:
                if ("tas", L, c // 2) not in M:
                    M["tas", L, c // 2] = psum.tile([P, 2, n], F32, name="tas", tag="x")
                acc = M["ta", L, c] = M["tas", L, c // 2][:, c % 2, :]
            pe.matmul_mx(
                out=acc[:, :], lhsT=w2_q[:, P * c:P * (c + 1)].bitcast(FP8X4), lhsT_scale=w2_s[:, P * c:P * (c + 1)],
                rhs=hidden_q[:, a:a + n].bitcast(FP8X4), rhs_scale=hidden_s[:, a:a + n], start=True, stop=True)

        def tl_step(L, c):
            low = M["low", L, c] = work.tile([P, G], F32, name="low", tag="low", bufs=5)
            sca.activation(out=low[:, 0:LG[L][1]], in_=M["ta", L, c][:, :], func=ACT.Identity, scale=SLOPE, bias=b2_s[:, c:c + 1])

        def tx_step(L, c):
            n = LG[L][1]
            top = M["top", L, c] = work.tile([P, G], F32, name="top", tag="top", bufs=6)
            vec.scalar_tensor_tensor(out=top[:, 0:n], in0=M["ta", L, c][:, :], scalar=b2_c[:, c:c + 1], in1=M["low", L, c][:, 0:n], op0=ALU.add, op1=ALU.max)

        def tb_step(L, i):
            back = M["back", L, i] = psum.tile([P, C], F32, name="back", tag="a")
            for c in range(4):
                pe.transpose(back[:, P * c:P * (c + 1)], M["top", L, c][:, P * i:P * (i + 1)], ident_f[:])

        def to_step(L, i):
            tile = LG[L][0] // P + i
            sca.copy(out=o4[:, tile, :], in_=M["back", L, i][:])
            put(tile)

        def nm_step(L, i):
            a = LG[L][0] + P * i
            acc = M["na", L, i] = psum.tile([P, C], F32, name="acc2", tag="x")
            pe.matmul_mx(
                out=acc[:], lhsT=hidden_q[:, a:a + P].bitcast(FP8X4), lhsT_scale=hidden_s[:, a:a + P],
                rhs=w2_q[:].bitcast(FP8X4), rhs_scale=w2_s[:], start=True, stop=True)

        def na_step(L, i):
            v2 = M["v2", L, i] = work.tile([P, C], F32, name="v2", tag="v2", bufs=4)
            vec.tensor_tensor(out=v2[:], in0=M["na", L, i][:], in1=b2_t[:], op=ALU.add)

        def no_step(L, i):
            v2 = M["v2", L, i]
            tile = LG[L][0] // P + i
            vec.scalar_tensor_tensor(out=o4[:, tile, :], in0=v2[:], scalar=SLOPE, in1=v2[:], op0=ALU.mult, op1=ALU.max)
            put(tile)

        for g in ("F", 0, 1, 2):
            S["y%s" % g] = lambda g=g: y_step(g)
            S["k%s" % g] = lambda g=g: k_step(g)
            S["f%s" % g] = lambda g=g: f_step(g)
        S["sF"] = lambda: sin_step("F")
        for L in range(len(LG)):
            S["s%d" % L] = lambda L=L: sin_step(L)
            S["q1%d" % L] = lambda L=L: q_step(1, L)
            S["q0%d" % L] = lambda L=L: q_step(0, L)
            S["h%d" % L] = lambda L=L: h_step(L)
            S["qh%d" % L] = lambda L=L: qh_step(L)
            for c in range(4):
                S["m%d%d" % (L, c)] = lambda L=L, c=c: m1_step(L, c)
                S["v%d%d" % (L, c)] = lambda L=L, c=c: v1_step(L, c)
                if L in TURNED:
                    S["tm%d%d" % (L, c)] = lambda L=L, c=c: tm_step(L, c)
                    S["tl%d%d" % (L, c)] = lambda L=L, c=c: tl_step(L, c)
                    S["tx%d%d" % (L, c)] = lambda L=L, c=c: tx_step(L, c)
            for i in range(LG[L][1] // P):
                if L in TURNED:
                    S["tb%d%d" % (L, i)] = lambda L=L, i=i: tb_step(L, i)
                    S["to%d%d" % (L, i)] = lambda L=L, i=i: to_step(L, i)
                else:
                    S["nm%d%d" % (L, i)] = lambda L=L, i=i: nm_step(L, i)
                    S["na%d%d" % (L, i)] = lambda L=L, i=i: na_step(L, i)
                    S["no%d%d" % (L, i)] = lambda L=L, i=i: no_step(L, i)

        sca.activation(out=warm2[:], in_=warm[:], func=ACT.Sin)
        for name in ORDER.split():
            S[name]()
